import numpy as np
import ml_dtypes


def mxq(x, axis, fmt="e4m3"):
    dtype, down = {"e4m3": (ml_dtypes.float8_e4m3fn, 7), "e5m2": (ml_dtypes.float8_e5m2, 14)}[fmt]
    v = np.moveaxis(np.asarray(x, np.float32).astype(ml_dtypes.bfloat16).astype(np.float64), axis, -1)
    blocks = v.reshape(v.shape[:-1] + (-1, 32))
    amax = np.abs(blocks).max(-1, keepdims=True)
    byte = np.maximum(np.where(amax > 0, np.frexp(amax)[1] - 1 + 127, 0) - down, 1)
    scale = np.exp2(byte - 127.0)
    codes = (blocks / scale).astype(np.float32).astype(dtype).astype(np.float64)
    return np.moveaxis((codes * scale).reshape(v.shape), -1, axis)


WIDE = False


def mx_kscale(k):
    if not WIDE:
        return np.ones(k)
    levels = np.array([10, -10, 5, -5, 0])
    a = np.random.permutation(np.resize(levels, k // 512 * 4)).reshape(k // 512, 4)
    idx = np.arange(k)
    return np.exp2(a[idx // 512, idx % 128 // 32])


BF16 = ml_dtypes.bfloat16


def bf(x):
    return np.asarray(x, np.float32).astype(BF16)


def f64(x):
    return np.asarray(x).astype(np.float64)


B, C, H, W = 16, 512, 16, 32
C2 = C // 2
N = H * W


def sigmoid(v):
    return 1.0 / (1.0 + np.exp(-v))


def setup_inputs():
    s = mx_kscale(C)
    amp = 0.4 + 1.2 * np.random.random((B, 1, H, W))
    return {
        'x1': bf(np.random.standard_normal((B, C, H, W)) * amp * s[None, :, None, None]),
        'wq1': bf(np.random.standard_normal((C2, C)) * 0.7 / np.sqrt(C) / s[None, :]),
        'bq1': bf(np.random.standard_normal(C2) * 0.3),
        'wv1': bf(np.random.standard_normal((C2, C)) * 6.0 / np.sqrt(N * C) / s[None, :]),
        'bv1': bf(np.random.standard_normal(C2) * 6.0 / N),
        'k2': bf(np.random.standard_normal((B, N)) * 0.8),
    }


def reference(x1, wq1, bq1, wv1, bv1, k2):
    xq = mxq(f64(x1).reshape(B, C, N), 1, 'e4m3')
    q1 = ((mxq(f64(wq1), 1, 'e4m3') @ xq) + f64(bq1)[None, :, None]).max(axis=1)
    v1 = (mxq(f64(wv1), 1, 'e4m3') @ xq) + f64(bv1)[None, :, None]
    att2 = 1.0 - sigmoid(q1[:, :, None] * f64(k2)[:, None, :])
    out = mxq(v1, 2, 'e4m3') @ mxq(att2, 2, 'e4m3').transpose(0, 2, 1)
    return out.reshape(B, C2, H, W)

@@ -1,0 +1,304 @@
+from contextlib import ExitStack
+
+import concourse.mybir as mybir
+from concourse.masks import make_identity
+
+F32 = mybir.dt.float32
+BF16 = mybir.dt.bfloat16
+U32 = mybir.dt.uint32
+U8 = mybir.dt.uint8
+FP8X4 = mybir.dt.float8_e4m3fn_x4
+ACT = mybir.ActivationFunctionType
+ALU = mybir.AluOpType
+AXIS = mybir.AxisListType
+
+B = 16
+C = 512
+C2 = 256
+N = 512
+P = 128
+PACK = 4
+TILES = N // P
+HALVES = C2 // P
+
+FLOPS = 2 * B * (2 * C2 * C * N + C2 * N * N)
+
+
+def tile_cross_module_pa_t_kernel(tc, x1, wq1, bq1, wv1, bv1, k2, out):
+    nc = tc.nc
+    with ExitStack() as stack:
+        stack.enter_context(tc.manual_schedule())
+        const = stack.enter_context(tc.tile_pool(name="const", bufs=1))
+        xin = stack.enter_context(tc.tile_pool(name="xin", bufs=B))
+        work = stack.enter_context(tc.tile_pool(name="work", bufs=2))
+
+        w_rows = const.tile([P, 2 * HALVES, C], BF16)
+        nc.sync.dma_start(out=w_rows[:, 0:HALVES, :], in_=wq1.rearrange("(g o) c -> o g c", o=P))
+        nc.sync.dma_start(out=w_rows[:, HALVES:, :], in_=wv1.rearrange("(g o) c -> o g c", o=P))
+
+        bias_rows = const.tile([P, P], BF16)
+        nc.vector.memset(bias_rows[:], 0.0)
+        bv_all = const.tile([P, C2], BF16)
+        k2_all = const.tile([P, B, N], BF16)
+
+        x_raw = {}
+
+        def load_x(b):
+            xr = xin.tile([P, PACK, N], BF16)
+            nc.sync.dma_start(
+                out=xr[:].rearrange("p (u e) n -> p u e n", u=2),
+                in_=x1[b].rearrange("(u p e) h w -> p u e (h w)", u=2, e=2),
+            )
+            x_raw[b] = xr
+
+        def load_k2(first, count):
+            nc.sync.dma_start(
+                out=k2_all[:, first : first + count, :].rearrange("p b n -> p (b n)"),
+                in_=k2[first : first + count, :].rearrange("b n -> (b n)").partition_broadcast(P),
+            )
+
+        nc.sync.dma_start(out=bias_rows[0:HALVES, :], in_=bq1.rearrange("(g o) -> g o", o=P))
+        load_x(0)
+        nc.sync.dma_start(out=bv_all[:], in_=bv1.partition_broadcast(P))
+        K2_BATCHES = 4
+        for b in range(1, B):
+            if (b - 1) % K2_BATCHES == 0:
+                load_k2(b - 1, K2_BATCHES)
+            load_x(b)
+
+        ident_f32 = const.tile([P, P], F32)
+        make_identity(nc, ident_f32[:])
+        ident_bf16 = const.tile([P, P], BF16)
+        make_identity(nc, ident_bf16[:])
+
+        warm = const.tile([P, 1], F32)
+        nc.vector.memset(warm[:], 0.0)
+        nc.scalar.activation(out=warm[:], in_=warm[:], func=ACT.Sigmoid)
+
+        w_words = w_rows[:].rearrange("o g c -> o (g c)").bitcast(F32)
+        WORDS = C // 2
+        w_grouped = const.tile([P, 2 * C2 * PACK], BF16, align_bytes=64)
+        w_grouped_words = w_grouped[:].bitcast(F32).rearrange("p (col u) -> p col u", u=2)
+        w_codes = const.tile([P, 2 * C2], U32, align_bytes=64)
+        w_scales = const.tile([P, 2 * C2], U8, align_bytes=64)
+        bq_cols = const.tile([P, HALVES], F32)
+        with tc.psum_pool(name="setup_psum", bufs=1) as setup_psum:
+            wqT = setup_psum.tile([P, 2, C2], F32)
+            wvT = setup_psum.tile([P, 2, C2], F32)
+            for i, wT in enumerate((wqT, wvT)):
+                for g in range(HALVES):
+                    for u in range(2):
+                        first = (i * HALVES + g) * WORDS + u * P
+                        nc.tensor.transpose(
+                            wT[:, u, g * P : (g + 1) * P], w_words[:, first : first + P], ident_f32[:]
+                        )
+            bqT = setup_psum.tile([P, P], BF16)
+            nc.tensor.transpose(bqT[:], bias_rows[:], ident_bf16[:])
+            nc.vector.tensor_copy(
+                out=w_grouped_words[:, 0:C2, :], in_=wqT[:].rearrange("p u col -> p col u")
+            )
+            nc.scalar.copy(
+                out=w_grouped_words[:, C2:, :], in_=wvT[:].rearrange("p u col -> p col u")
+            )
+            nc.vector.tensor_copy(out=bq_cols[:], in_=bqT[:, 0:HALVES])
+        nc.vector.quantize_mx(out=w_codes[:].bitcast(FP8X4), scales=w_scales[:], in_=w_grouped[:])
+
+        psum = stack.enter_context(tc.psum_pool(name="psum", bufs=1))
+        x_grouped, x_codes, x_scales = {}, {}, {}
+        q_lo, q_hi, q_hi_biased, q_max, q_maxT, neg_q1 = {}, {}, {}, {}, {}, {}
+        vT, v_grouped, v_codes, v_scales = {}, {}, {}, {}
+        gate, gateT, gate_grouped, gate_codes, gate_scales = {}, {}, {}, {}, {}
+        product, result = {}, {}
+
+        def regroup_x(b):
+            xg = work.tile([P, N, PACK], BF16, align_bytes=64)
+            nc.vector.tensor_copy(
+                out=xg[:].rearrange("p (c i) t -> p c t i", i=4),
+                in_=x_raw[b][:].rearrange("p t (c i) -> p c t i", i=4),
+            )
+            x_grouped[b] = xg
+
+        def quantise_x(b):
+            xc = work.tile([P, N], U32, align_bytes=64)
+            xs = work.tile([P, N], U8, align_bytes=64)
+            nc.vector.quantize_mx(
+                out=xc[:].bitcast(FP8X4),
+                scales=xs[:],
+                in_=x_grouped[b][:].rearrange("p n t -> p (n t)"),
+            )
+            x_codes[b], x_scales[b] = xc, xs
+
+        def project(b):
+            xc, xs = x_codes[b], x_scales[b]
+            lo = psum.tile([P, N], F32, tag="q_lo")
+            hi = psum.tile([P, N], F32, tag="q_hi")
+            for g, acc in enumerate((lo, hi)):
+                cols = slice(g * P, (g + 1) * P)
+                nc.tensor.matmul_mx(
+                    out=acc[:],
+                    lhsT=w_codes[:, cols].bitcast(FP8X4),
+                    lhsT_scale=w_scales[:, cols],
+                    rhs=xc[:].bitcast(FP8X4),
+                    rhs_scale=xs[:],
+                    start=True,
+                    stop=True,
+                )
+            q_lo[b], q_hi[b] = lo, hi
+            for h in range(HALVES):
+                acc = psum.tile([P, TILES, P], F32, tag="vT%d" % h, name="vT%d" % h)
+                w_cols = slice(C2 + h * P, C2 + (h + 1) * P)
+                for t in range(TILES):
+                    x_cols = slice(t * P, (t + 1) * P)
+                    nc.tensor.matmul_mx(
+                        out=acc[:, t, :],
+                        lhsT=xc[:, x_cols].bitcast(FP8X4),
+                        lhsT_scale=xs[:, x_cols],
+                        rhs=w_codes[:, w_cols].bitcast(FP8X4),
+                        rhs_scale=w_scales[:, w_cols],
+                        start=True,
+                        stop=True,
+                    )
+                vT[b, h] = acc
+
+        def bias_q_hi(b):
+            qb = work.tile([P, N], F32)
+            nc.scalar.activation(
+                out=qb[:], in_=q_hi[b][:], func=ACT.Identity, bias=bq_cols[:, 1:2], scale=1.0
+            )
+            q_hi_biased[b] = qb
+
+        def max_of_halves(b):
+            qm = work.tile([P, N], F32)
+            nc.vector.scalar_tensor_tensor(
+                out=qm[:],
+                in0=q_lo[b][:],
+                scalar=bq_cols[:, 0:1],
+                in1=q_hi_biased[b][:],
+                op0=ALU.add,
+                op1=ALU.max,
+            )
+            q_max[b] = qm
+
+        def transpose_q(b):
+            qT = psum.tile([P, TILES, P], F32, tag="q_hi")
+            for t in range(TILES):
+                nc.tensor.transpose(qT[:, t, :], q_max[b][:, t * P : (t + 1) * P], ident_f32[:])
+            q_maxT[b] = qT
+
+        def max_over_channels(b):
+            nq = work.tile([P, TILES], F32, bufs=3)
+            nc.vector.tensor_reduce(
+                out=nq[:], in_=q_maxT[b][:], axis=AXIS.X, op=ALU.max, negate=True
+            )
+            neg_q1[b] = nq
+
+        def bias_v(b):
+            vg = work.tile([P, C2, PACK], BF16, align_bytes=64)
+            for h in range(HALVES):
+                cols = slice(h * P, (h + 1) * P)
+                nc.vector.tensor_tensor(
+                    out=vg[:, cols, :],
+                    in0=vT[b, h][:].rearrange("p t c -> p c t"),
+                    in1=bv_all[:, cols].unsqueeze(2).to_broadcast([P, P, PACK]),
+                    op=ALU.add,
+                )
+            v_grouped[b] = vg
+
+        def quantise_v(b):
+            vc = work.tile([P, C2], U32, align_bytes=64, bufs=3)
+            vs = work.tile([P, C2], U8, align_bytes=64, bufs=3)
+            nc.vector.quantize_mx(
+                out=vc[:].bitcast(FP8X4),
+                scales=vs[:],
+                in_=v_grouped[b][:].rearrange("p c t -> p (c t)"),
+            )
+            v_codes[b], v_scales[b] = vc, vs
+
+        def gate_rows(b):
+            ga = work.tile([P, TILES, N], BF16)
+            for t in range(TILES):
+                nc.scalar.activation(
+                    out=ga[:, t, :].rearrange("p (u q e) -> p u q e", u=2, e=2),
+                    in_=k2_all[:, b, :].rearrange("p (u e q) -> p u q e", u=2, e=2),
+                    func=ACT.Sigmoid,
+                    scale=neg_q1[b][:, t : t + 1],
+                )
+            gate[b] = ga
+
+        def transpose_gate(b):
+            words = gate[b][:].rearrange("p t k -> p (t k)").bitcast(F32)
+            for h in range(2):
+                gT = psum.tile([P, 2, 2 * P], F32, tag="gateT%d" % h, name="gateT%d" % h)
+                for j in range(2):
+                    for u in range(2):
+                        first = (2 * h + j) * (N // 2) + u * P
+                        nc.tensor.transpose(
+                            gT[:, u, j * P : (j + 1) * P], words[:, first : first + P], ident_f32[:]
+                        )
+                gateT[b, h] = gT
+
+        def new_gate_grouped(b):
+            gg = work.tile([P, N * PACK], BF16, align_bytes=64)
+            gate_grouped[b] = gg
+
+        def regroup_gate(b, h):
+            words = gate_grouped[b][:].bitcast(F32).rearrange("p (m u) -> p m u", u=2)
+            nc.scalar.copy(
+                out=words[:, h * 2 * P : (h + 1) * 2 * P, :],
+                in_=gateT[b, h][:].rearrange("p u m -> p m u"),
+            )
+
+        def quantise_gate(b):
+            gc = work.tile([P, N], U32, align_bytes=64)
+            gs = work.tile([P, N], U8, align_bytes=64)
+            nc.vector.quantize_mx(out=gc[:].bitcast(FP8X4), scales=gs[:], in_=gate_grouped[b][:])
+            gate_codes[b], gate_scales[b] = gc, gs
+
+        def multiply(b):
+            for g in range(HALVES):
+                acc = psum.tile([P, N], F32, tag="out%d" % g, name="out%d" % g)
+                cols = slice(g * P, (g + 1) * P)
+                nc.tensor.matmul_mx(
+                    out=acc[:],
+                    lhsT=v_codes[b][:, cols].bitcast(FP8X4),
+                    lhsT_scale=v_scales[b][:, cols],
+                    rhs=gate_codes[b][:].bitcast(FP8X4),
+                    rhs_scale=gate_scales[b][:],
+                    start=True,
+                    stop=True,
+                )
+                product[b, g] = acc
+            res = work.tile([P, HALVES, N], F32, bufs=4)
+            result[b] = res
+
+        def store(b):
+            nc.sync.dma_start(
+                out=out[b].rearrange("(g c) h w -> c g (h w)", c=P), in_=result[b][:]
+            )
+
+        def when(b, stage, *args):
+            if 0 <= b < B:
+                stage(b, *args)
+
+        for s in range(-3, B + 1):
+            when(s - 1, quantise_gate)
+            when(s - 1, multiply)
+            when(s + 1, bias_q_hi)
+            when(s + 1, max_of_halves)
+            when(s + 1, transpose_q)
+            when(s + 1, bias_v)
+            when(s + 1, max_over_channels)
+            when(s + 1, quantise_v)
+            when(s, gate_rows)
+            when(s, transpose_gate)
+            when(s, new_gate_grouped)
+            when(s, regroup_gate, 0)
+            if 0 <= s - 1 < B:
+                nc.scalar.copy(out=result[s - 1][:, 0, :], in_=product[s - 1, 0][:])
+            when(s, regroup_gate, 1)
+            when(s + 2, quantise_x)
+            when(s + 2, project)
+            when(s + 3, regroup_x)
+            if 0 <= s - 1 < B:
+                nc.vector.tensor_copy(out=result[s - 1][:, 1, :], in_=product[s - 1, 1][:])
+            when(s - 1, store)

@@ -20,6 +20,8 @@ P = 128
 PACK = 4
 TILES = N // P
 HALVES = C2 // P
+WORDS = C // 2
+K2_BATCHES = 4
 
 FLOPS = 2 * B * (2 * C2 * C * N + C2 * N * N)
 
@@ -40,7 +42,6 @@ def tile_cross_module_pa_t_kernel(tc, x1, wq1, bq1, wv1, bv1, k2, out):
         nc.vector.memset(bias_rows[:], 0.0)
         bv_all = const.tile([P, C2], BF16)
         k2_all = const.tile([P, B, N], BF16)
-
         x_raw = {}
 
         def load_x(b):
@@ -60,7 +61,6 @@ def tile_cross_module_pa_t_kernel(tc, x1, wq1, bq1, wv1, bv1, k2, out):
         nc.sync.dma_start(out=bias_rows[0:HALVES, :], in_=bq1.rearrange("(g o) -> g o", o=P))
         load_x(0)
         nc.sync.dma_start(out=bv_all[:], in_=bv1.partition_broadcast(P))
-        K2_BATCHES = 4
         for b in range(1, B):
             if (b - 1) % K2_BATCHES == 0:
                 load_k2(b - 1, K2_BATCHES)
@@ -75,35 +75,33 @@ def tile_cross_module_pa_t_kernel(tc, x1, wq1, bq1, wv1, bv1, k2, out):
         nc.vector.memset(warm[:], 0.0)
         nc.scalar.activation(out=warm[:], in_=warm[:], func=ACT.Sigmoid)
 
-        w_words = w_rows[:].rearrange("o g c -> o (g c)").bitcast(F32)
-        WORDS = C // 2
         w_grouped = const.tile([P, 2 * C2 * PACK], BF16, align_bytes=64)
-        w_grouped_words = w_grouped[:].bitcast(F32).rearrange("p (col u) -> p col u", u=2)
         w_codes = const.tile([P, 2 * C2], U32, align_bytes=64)
         w_scales = const.tile([P, 2 * C2], U8, align_bytes=64)
         bq_cols = const.tile([P, HALVES], F32)
-        with tc.psum_pool(name="setup_psum", bufs=1) as setup_psum:
-            wqT = setup_psum.tile([P, 2, C2], F32)
-            wvT = setup_psum.tile([P, 2, C2], F32)
-            for i, wT in enumerate((wqT, wvT)):
-                for g in range(HALVES):
-                    for u in range(2):
-                        first = (i * HALVES + g) * WORDS + u * P
-                        nc.tensor.transpose(
-                            wT[:, u, g * P : (g + 1) * P], w_words[:, first : first + P], ident_f32[:]
-                        )
-            bqT = setup_psum.tile([P, P], BF16)
-            nc.tensor.transpose(bqT[:], bias_rows[:], ident_bf16[:])
-            nc.vector.tensor_copy(
-                out=w_grouped_words[:, 0:C2, :], in_=wqT[:].rearrange("p u col -> p col u")
-            )
-            nc.scalar.copy(
-                out=w_grouped_words[:, C2:, :], in_=wvT[:].rearrange("p u col -> p col u")
-            )
-            nc.vector.tensor_copy(out=bq_cols[:], in_=bqT[:, 0:HALVES])
-        nc.vector.quantize_mx(out=w_codes[:].bitcast(FP8X4), scales=w_scales[:], in_=w_grouped[:])
 
-        psum = stack.enter_context(tc.psum_pool(name="psum", bufs=1))
+        def transpose_weights():
+            w_words = w_rows[:].rearrange("o g c -> o (g c)").bitcast(F32)
+            grouped_words = w_grouped[:].bitcast(F32).rearrange("p (col u) -> p col u", u=2)
+            with tc.psum_pool(name="setup_psum", bufs=1) as setup_psum:
+                for i in range(2):
+                    wT = setup_psum.tile([P, 2, C2], F32, name="wT%d" % i)
+                    for g in range(HALVES):
+                        for u in range(2):
+                            first = (i * HALVES + g) * WORDS + u * P
+                            nc.tensor.transpose(
+                                wT[:, u, g * P : (g + 1) * P],
+                                w_words[:, first : first + P],
+                                ident_f32[:],
+                            )
+                    nc.scalar.copy(
+                        out=grouped_words[:, i * C2 : (i + 1) * C2, :],
+                        in_=wT[:].rearrange("p u col -> p col u"),
+                    )
+                bqT = setup_psum.tile([P, P], BF16)
+                nc.tensor.transpose(bqT[:], bias_rows[:], ident_bf16[:])
+                nc.scalar.copy(out=bq_cols[:], in_=bqT[:, 0:HALVES])
+
         x_grouped, x_codes, x_scales = {}, {}, {}
         q_lo, q_hi, q_hi_biased, q_max, q_maxT, neg_q1 = {}, {}, {}, {}, {}, {}
         vT, v_grouped, v_codes, v_scales = {}, {}, {}, {}
@@ -128,8 +126,24 @@ def tile_cross_module_pa_t_kernel(tc, x1, wq1, bq1, wv1, bv1, k2, out):
             )
             x_codes[b], x_scales[b] = xc, xs
 
-        def project(b):
-            xc, xs = x_codes[b], x_scales[b]
+        def project_v(b):
+            for h in range(HALVES):
+                acc = psum.tile([P, TILES, P], F32, tag="vT%d" % h, name="vT%d" % h)
+                w_cols = slice(C2 + h * P, C2 + (h + 1) * P)
+                for t in range(TILES):
+                    x_cols = slice(t * P, (t + 1) * P)
+                    nc.tensor.matmul_mx(
+                        out=acc[:, t, :],
+                        lhsT=x_codes[b][:, x_cols].bitcast(FP8X4),
+                        lhsT_scale=x_scales[b][:, x_cols],
+                        rhs=w_codes[:, w_cols].bitcast(FP8X4),
+                        rhs_scale=w_scales[:, w_cols],
+                        start=True,
+                        stop=True,
+                    )
+                vT[b, h] = acc
+
+        def project_q(b):
             lo = psum.tile([P, N], F32, tag="q_lo")
             hi = psum.tile([P, N], F32, tag="q_hi")
             for g, acc in enumerate((lo, hi)):
@@ -138,27 +152,12 @@ def tile_cross_module_pa_t_kernel(tc, x1, wq1, bq1, wv1, bv1, k2, out):
                     out=acc[:],
                     lhsT=w_codes[:, cols].bitcast(FP8X4),
                     lhsT_scale=w_scales[:, cols],
-                    rhs=xc[:].bitcast(FP8X4),
-                    rhs_scale=xs[:],
+                    rhs=x_codes[b][:].bitcast(FP8X4),
+                    rhs_scale=x_scales[b][:],
                     start=True,
                     stop=True,
                 )
             q_lo[b], q_hi[b] = lo, hi
-            for h in range(HALVES):
-                acc = psum.tile([P, TILES, P], F32, tag="vT%d" % h, name="vT%d" % h)
-                w_cols = slice(C2 + h * P, C2 + (h + 1) * P)
-                for t in range(TILES):
-                    x_cols = slice(t * P, (t + 1) * P)
-                    nc.tensor.matmul_mx(
-                        out=acc[:, t, :],
-                        lhsT=xc[:, x_cols].bitcast(FP8X4),
-                        lhsT_scale=xs[:, x_cols],
-                        rhs=w_codes[:, w_cols].bitcast(FP8X4),
-                        rhs_scale=w_scales[:, w_cols],
-                        start=True,
-                        stop=True,
-                    )
-                vT[b, h] = acc
 
         def bias_q_hi(b):
             qb = work.tile([P, N], F32)
@@ -214,34 +213,33 @@ def tile_cross_module_pa_t_kernel(tc, x1, wq1, bq1, wv1, bv1, k2, out):
             )
             v_codes[b], v_scales[b] = vc, vs
 
-        def gate_rows(b):
-            ga = work.tile([P, TILES, N], BF16)
-            for t in range(TILES):
+        def gate_rows(b, h):
+            if h == 0:
+                ga = work.tile([P, TILES, N], BF16)
+                gate[b] = ga
+            for t in (2 * h, 2 * h + 1):
                 nc.scalar.activation(
-                    out=ga[:, t, :].rearrange("p (u q e) -> p u q e", u=2, e=2),
+                    out=gate[b][:, t, :].rearrange("p (u q e) -> p u q e", u=2, e=2),
                     in_=k2_all[:, b, :].rearrange("p (u e q) -> p u q e", u=2, e=2),
                     func=ACT.Sigmoid,
                     scale=neg_q1[b][:, t : t + 1],
                 )
-            gate[b] = ga
 
-        def transpose_gate(b):
+        def transpose_gate(b, h):
             words = gate[b][:].rearrange("p t k -> p (t k)").bitcast(F32)
-            for h in range(2):
-                gT = psum.tile([P, 2, 2 * P], F32, tag="gateT%d" % h, name="gateT%d" % h)
-                for j in range(2):
-                    for u in range(2):
-                        first = (2 * h + j) * (N // 2) + u * P
-                        nc.tensor.transpose(
-                            gT[:, u, j * P : (j + 1) * P], words[:, first : first + P], ident_f32[:]
-                        )
-                gateT[b, h] = gT
-
-        def new_gate_grouped(b):
-            gg = work.tile([P, N * PACK], BF16, align_bytes=64)
-            gate_grouped[b] = gg
+            gT = psum.tile([P, 2, 2 * P], F32, tag="gateT%d" % h, name="gateT%d" % h)
+            for j in range(2):
+                for u in range(2):
+                    first = (2 * h + j) * WORDS + u * P
+                    nc.tensor.transpose(
+                        gT[:, u, j * P : (j + 1) * P], words[:, first : first + P], ident_f32[:]
+                    )
+            gateT[b, h] = gT
 
         def regroup_gate(b, h):
+            if h == 0:
+                gg = work.tile([P, N * PACK], BF16, align_bytes=64)
+                gate_grouped[b] = gg
             words = gate_grouped[b][:].bitcast(F32).rearrange("p (m u) -> p m u", u=2)
             nc.scalar.copy(
                 out=words[:, h * 2 * P : (h + 1) * 2 * P, :],
@@ -268,37 +266,40 @@ def tile_cross_module_pa_t_kernel(tc, x1, wq1, bq1, wv1, bv1, k2, out):
                     stop=True,
                 )
                 product[b, g] = acc
-            res = work.tile([P, HALVES, N], F32, bufs=4)
-            result[b] = res
 
         def store(b):
-            nc.sync.dma_start(
-                out=out[b].rearrange("(g c) h w -> c g (h w)", c=P), in_=result[b][:]
-            )
+            res = work.tile([P, HALVES, N], F32, bufs=4)
+            for g in range(HALVES):
+                nc.scalar.copy(out=res[:, g, :], in_=product[b, g][:])
+            nc.sync.dma_start(out=out[b].rearrange("(g c) h w -> c g (h w)", c=P), in_=res[:])
+
+        regroup_x(0)
+        transpose_weights()
+        nc.vector.quantize_mx(out=w_codes[:].bitcast(FP8X4), scales=w_scales[:], in_=w_grouped[:])
+
+        psum = stack.enter_context(tc.psum_pool(name="psum", bufs=1))
 
         def when(b, stage, *args):
             if 0 <= b < B:
                 stage(b, *args)
 
-        for s in range(-3, B + 1):
+        for s in range(-2, B + 1):
             when(s - 1, quantise_gate)
             when(s - 1, multiply)
+            when(s, quantise_v)
+            when(s + 2, quantise_x)
+            when(s, gate_rows, 0)
+            when(s, transpose_gate, 0)
             when(s + 1, bias_q_hi)
             when(s + 1, max_of_halves)
             when(s + 1, transpose_q)
+            when(s, gate_rows, 1)
+            when(s, transpose_gate, 1)
             when(s + 1, bias_v)
             when(s + 1, max_over_channels)
-            when(s + 1, quantise_v)
-            when(s, gate_rows)
-            when(s, transpose_gate)
-            when(s, new_gate_grouped)
             when(s, regroup_gate, 0)
-            if 0 <= s - 1 < B:
-                nc.scalar.copy(out=result[s - 1][:, 0, :], in_=product[s - 1, 0][:])
-            when(s, regroup_gate, 1)
-            when(s + 2, quantise_x)
-            when(s + 2, project)
-            when(s + 3, regroup_x)
-            if 0 <= s - 1 < B:
-                nc.vector.tensor_copy(out=result[s - 1][:, 1, :], in_=product[s - 1, 1][:])
             when(s - 1, store)
+            when(s, regroup_gate, 1)
+            when(s + 2, project_v)
+            when(s + 2, project_q)
+            when(s + 3, regroup_x)

@@ -22,6 +22,7 @@ TILES = N // P
 HALVES = C2 // P
 WORDS = C // 2
 K2_BATCHES = 4
+VECTOR_REGROUPS = 2
 
 FLOPS = 2 * B * (2 * C2 * C * N + C2 * N * N)
 
@@ -110,10 +111,20 @@ def tile_cross_module_pa_t_kernel(tc, x1, wq1, bq1, wv1, bv1, k2, out):
 
         def regroup_x(b):
             xg = work.tile([P, N, PACK], BF16, align_bytes=64)
-            nc.vector.tensor_copy(
-                out=xg[:].rearrange("p (c i) t -> p c t i", i=4),
-                in_=x_raw[b][:].rearrange("p t (c i) -> p c t i", i=4),
-            )
+            if b < VECTOR_REGROUPS:
+                nc.vector.tensor_copy(
+                    out=xg[:].rearrange("p (c i) t -> p c t i", i=4),
+                    in_=x_raw[b][:].rearrange("p t (c i) -> p c t i", i=4),
+                )
+            else:
+                nc.gpsimd.tensor_scalar(
+                    out=xg[:],
+                    in0=x_raw[b][:].rearrange("p t n -> p n t"),
+                    scalar1=1.0,
+                    scalar2=0.0,
+                    op0=ALU.mult,
+                    op1=ALU.add,
+                )
             x_grouped[b] = xg
 
         def quantise_x(b):

@@ -21,7 +21,6 @@ PACK = 4
 TILES = N // P
 HALVES = C2 // P
 WORDS = C // 2
-K2_BATCHES = 4
 VECTOR_REGROUPS = 2
 
 FLOPS = 2 * B * (2 * C2 * C * N + C2 * N * N)
@@ -42,7 +41,8 @@ def tile_cross_module_pa_t_kernel(tc, x1, wq1, bq1, wv1, bv1, k2, out):
         bias_rows = const.tile([P, P], BF16)
         nc.vector.memset(bias_rows[:], 0.0)
         bv_all = const.tile([P, C2], BF16)
-        k2_all = const.tile([P, B, N], BF16)
+        k2_rows = const.tile([P, N], BF16)
+        nc.vector.memset(k2_rows[:], 0.0)
         x_raw = {}
 
         def load_x(b):
@@ -53,18 +53,11 @@ def tile_cross_module_pa_t_kernel(tc, x1, wq1, bq1, wv1, bv1, k2, out):
             )
             x_raw[b] = xr
 
-        def load_k2(first, count):
-            nc.sync.dma_start(
-                out=k2_all[:, first : first + count, :].rearrange("p b n -> p (b n)"),
-                in_=k2[first : first + count, :].rearrange("b n -> (b n)").partition_broadcast(P),
-            )
-
+        nc.sync.dma_start(out=k2_rows[0:B, :], in_=k2)
         nc.sync.dma_start(out=bias_rows[0:HALVES, :], in_=bq1.rearrange("(g o) -> g o", o=P))
         load_x(0)
         nc.sync.dma_start(out=bv_all[:], in_=bv1.partition_broadcast(P))
         for b in range(1, B):
-            if (b - 1) % K2_BATCHES == 0:
-                load_k2(b - 1, K2_BATCHES)
             load_x(b)
 
         ident_f32 = const.tile([P, P], F32)
@@ -106,8 +99,9 @@ def tile_cross_module_pa_t_kernel(tc, x1, wq1, bq1, wv1, bv1, k2, out):
         x_grouped, x_codes, x_scales = {}, {}, {}
         q_lo, q_hi, q_hi_biased, q_max, q_maxT, neg_q1 = {}, {}, {}, {}, {}, {}
         vT, v_grouped, v_codes, v_scales = {}, {}, {}, {}
+        k2_spread, k2_kept = {}, {}
         gate, gateT, gate_grouped, gate_codes, gate_scales = {}, {}, {}, {}, {}
-        product, result = {}, {}
+        product = {}
 
         def regroup_x(b):
             xg = work.tile([P, N, PACK], BF16, align_bytes=64)
@@ -137,38 +131,35 @@ def tile_cross_module_pa_t_kernel(tc, x1, wq1, bq1, wv1, bv1, k2, out):
             )
             x_codes[b], x_scales[b] = xc, xs
 
-        def project_v(b):
-            for h in range(HALVES):
-                acc = psum.tile([P, TILES, P], F32, tag="vT%d" % h, name="vT%d" % h)
-                w_cols = slice(C2 + h * P, C2 + (h + 1) * P)
-                for t in range(TILES):
-                    x_cols = slice(t * P, (t + 1) * P)
-                    nc.tensor.matmul_mx(
-                        out=acc[:, t, :],
-                        lhsT=x_codes[b][:, x_cols].bitcast(FP8X4),
-                        lhsT_scale=x_scales[b][:, x_cols],
-                        rhs=w_codes[:, w_cols].bitcast(FP8X4),
-                        rhs_scale=w_scales[:, w_cols],
-                        start=True,
-                        stop=True,
-                    )
-                vT[b, h] = acc
-
-        def project_q(b):
-            lo = psum.tile([P, N], F32, tag="q_lo")
-            hi = psum.tile([P, N], F32, tag="q_hi")
-            for g, acc in enumerate((lo, hi)):
-                cols = slice(g * P, (g + 1) * P)
+        def project_v(b, h):
+            acc = psum.tile([P, TILES, P], F32, tag="vT%d" % h, name="vT%d" % h)
+            w_cols = slice(C2 + h * P, C2 + (h + 1) * P)
+            for t in range(TILES):
+                x_cols = slice(t * P, (t + 1) * P)
                 nc.tensor.matmul_mx(
-                    out=acc[:],
-                    lhsT=w_codes[:, cols].bitcast(FP8X4),
-                    lhsT_scale=w_scales[:, cols],
-                    rhs=x_codes[b][:].bitcast(FP8X4),
-                    rhs_scale=x_scales[b][:],
+                    out=acc[:, t, :],
+                    lhsT=x_codes[b][:, x_cols].bitcast(FP8X4),
+                    lhsT_scale=x_scales[b][:, x_cols],
+                    rhs=w_codes[:, w_cols].bitcast(FP8X4),
+                    rhs_scale=w_scales[:, w_cols],
                     start=True,
                     stop=True,
                 )
-            q_lo[b], q_hi[b] = lo, hi
+            vT[b, h] = acc
+
+        def project_q(b, g):
+            acc = psum.tile([P, N], F32, tag=("q_lo", "q_hi")[g], name="q%d" % g)
+            cols = slice(g * P, (g + 1) * P)
+            nc.tensor.matmul_mx(
+                out=acc[:],
+                lhsT=w_codes[:, cols].bitcast(FP8X4),
+                lhsT_scale=w_scales[:, cols],
+                rhs=x_codes[b][:].bitcast(FP8X4),
+                rhs_scale=x_scales[b][:],
+                start=True,
+                stop=True,
+            )
+            (q_lo, q_hi)[g][b] = acc
 
         def bias_q_hi(b):
             qb = work.tile([P, N], F32)
@@ -190,7 +181,7 @@ def tile_cross_module_pa_t_kernel(tc, x1, wq1, bq1, wv1, bv1, k2, out):
             q_max[b] = qm
 
         def transpose_q(b):
-            qT = psum.tile([P, TILES, P], F32, tag="q_hi")
+            qT = psum.tile([P, TILES, P], F32, tag="q_lo")
             for t in range(TILES):
                 nc.tensor.transpose(qT[:, t, :], q_max[b][:, t * P : (t + 1) * P], ident_f32[:])
             q_maxT[b] = qT
@@ -202,17 +193,17 @@ def tile_cross_module_pa_t_kernel(tc, x1, wq1, bq1, wv1, bv1, k2, out):
             )
             neg_q1[b] = nq
 
-        def bias_v(b):
-            vg = work.tile([P, C2, PACK], BF16, align_bytes=64)
-            for h in range(HALVES):
-                cols = slice(h * P, (h + 1) * P)
-                nc.vector.tensor_tensor(
-                    out=vg[:, cols, :],
-                    in0=vT[b, h][:].rearrange("p t c -> p c t"),
-                    in1=bv_all[:, cols].unsqueeze(2).to_broadcast([P, P, PACK]),
-                    op=ALU.add,
-                )
-            v_grouped[b] = vg
+        def bias_v(b, h):
+            if h == 0:
+                vg = work.tile([P, C2, PACK], BF16, align_bytes=64)
+                v_grouped[b] = vg
+            cols = slice(h * P, (h + 1) * P)
+            nc.vector.tensor_tensor(
+                out=v_grouped[b][:, cols, :],
+                in0=vT[b, h][:].rearrange("p t c -> p c t"),
+                in1=bv_all[:, cols].unsqueeze(2).to_broadcast([P, P, PACK]),
+                op=ALU.add,
+            )
 
         def quantise_v(b):
             vc = work.tile([P, C2], U32, align_bytes=64, bufs=3)
@@ -224,6 +215,22 @@ def tile_cross_module_pa_t_kernel(tc, x1, wq1, bq1, wv1, bv1, k2, out):
             )
             v_codes[b], v_scales[b] = vc, vs
 
+        def spread_k2(b):
+            kb = psum.tile([P, N], BF16, tag="gateT1")
+            nc.tensor.matmul(
+                out=kb[:],
+                lhsT=ident_bf16[:, b : b + 1].to_broadcast([P, P]),
+                rhs=k2_rows[:],
+                start=True,
+                stop=True,
+            )
+            k2_spread[b] = kb
+
+        def keep_k2(b):
+            kk = work.tile([P, N], BF16, bufs=3)
+            nc.scalar.copy(out=kk[:], in_=k2_spread[b][:])
+            k2_kept[b] = kk
+
         def gate_rows(b, h):
             if h == 0:
                 ga = work.tile([P, TILES, N], BF16)
@@ -231,7 +238,7 @@ def tile_cross_module_pa_t_kernel(tc, x1, wq1, bq1, wv1, bv1, k2, out):
             for t in (2 * h, 2 * h + 1):
                 nc.scalar.activation(
                     out=gate[b][:, t, :].rearrange("p (u q e) -> p u q e", u=2, e=2),
-                    in_=k2_all[:, b, :].rearrange("p (u e q) -> p u q e", u=2, e=2),
+                    in_=k2_kept[b][:].rearrange("p (u e q) -> p u q e", u=2, e=2),
                     func=ACT.Sigmoid,
                     scale=neg_q1[b][:, t : t + 1],
                 )
@@ -278,11 +285,15 @@ def tile_cross_module_pa_t_kernel(tc, x1, wq1, bq1, wv1, bv1, k2, out):
                 )
                 product[b, g] = acc
 
-        def store(b):
-            res = work.tile([P, HALVES, N], F32, bufs=4)
-            for g in range(HALVES):
-                nc.scalar.copy(out=res[:, g, :], in_=product[b, g][:])
-            nc.sync.dma_start(out=out[b].rearrange("(g c) h w -> c g (h w)", c=P), in_=res[:])
+        def store(b, g):
+            res = work.tile([P, N], F32, bufs=8)
+            if g == 0:
+                nc.scalar.copy(out=res[:], in_=product[b, g][:])
+            else:
+                nc.vector.tensor_copy(out=res[:], in_=product[b, g][:])
+            nc.sync.dma_start(
+                out=out[b, g * P : (g + 1) * P].rearrange("c h w -> c (h w)"), in_=res[:]
+            )
 
         regroup_x(0)
         transpose_weights()
@@ -297,20 +308,26 @@ def tile_cross_module_pa_t_kernel(tc, x1, wq1, bq1, wv1, bv1, k2, out):
         for s in range(-2, B + 1):
             when(s - 1, quantise_gate)
             when(s - 1, multiply)
+            when(s + 1, bias_q_hi)
+            when(s + 1, max_of_halves)
             when(s, quantise_v)
             when(s + 2, quantise_x)
             when(s, gate_rows, 0)
             when(s, transpose_gate, 0)
-            when(s + 1, bias_q_hi)
-            when(s + 1, max_of_halves)
+            when(s + 1, keep_k2)
             when(s + 1, transpose_q)
             when(s, gate_rows, 1)
             when(s, transpose_gate, 1)
-            when(s + 1, bias_v)
+            when(s + 1, bias_v, 0)
             when(s + 1, max_over_channels)
+            when(s + 1, bias_v, 1)
             when(s, regroup_gate, 0)
-            when(s - 1, store)
+            when(s - 1, store, 0)
             when(s, regroup_gate, 1)
-            when(s + 2, project_v)
-            when(s + 2, project_q)
+            when(s - 1, store, 1)
+            when(s + 2, project_q, 1)
+            when(s + 2, project_v, 0)
+            when(s + 2, project_q, 0)
+            when(s + 2, project_v, 1)
+            when(s + 2, spread_k2)
             when(s + 3, regroup_x)

@@ -41,8 +41,7 @@ def tile_cross_module_pa_t_kernel(tc, x1, wq1, bq1, wv1, bv1, k2, out):
         bias_rows = const.tile([P, P], BF16)
         nc.vector.memset(bias_rows[:], 0.0)
         bv_all = const.tile([P, C2], BF16)
-        k2_rows = const.tile([P, N], BF16)
-        nc.vector.memset(k2_rows[:], 0.0)
+        k2_all = const.tile([P, B, N], BF16)
         x_raw = {}
 
         def load_x(b):
@@ -53,11 +52,22 @@ def tile_cross_module_pa_t_kernel(tc, x1, wq1, bq1, wv1, bv1, k2, out):
             )
             x_raw[b] = xr
 
-        nc.sync.dma_start(out=k2_rows[0:B, :], in_=k2)
+        def load_k2(first, last):
+            nc.sync.dma_start(
+                out=k2_all[:, first:last, :].rearrange("p b n -> p (b n)"),
+                in_=k2[first:last].rearrange("b n -> (b n)").partition_broadcast(P),
+            )
+
         nc.sync.dma_start(out=bias_rows[0:HALVES, :], in_=bq1.rearrange("(g o) -> g o", o=P))
         load_x(0)
         nc.sync.dma_start(out=bv_all[:], in_=bv1.partition_broadcast(P))
-        for b in range(1, B):
+        load_x(1)
+        load_k2(0, 2)
+        load_x(2)
+        load_k2(2, 4)
+        load_x(3)
+        load_k2(4, B)
+        for b in range(4, B):
             load_x(b)
 
         ident_f32 = const.tile([P, P], F32)
@@ -99,7 +109,6 @@ def tile_cross_module_pa_t_kernel(tc, x1, wq1, bq1, wv1, bv1, k2, out):
         x_grouped, x_codes, x_scales = {}, {}, {}
         q_lo, q_hi, q_hi_biased, q_max, q_maxT, neg_q1 = {}, {}, {}, {}, {}, {}
         vT, v_grouped, v_codes, v_scales = {}, {}, {}, {}
-        k2_spread, k2_kept = {}, {}
         gate, gateT, gate_grouped, gate_codes, gate_scales = {}, {}, {}, {}, {}
         product = {}
 
@@ -215,22 +224,6 @@ def tile_cross_module_pa_t_kernel(tc, x1, wq1, bq1, wv1, bv1, k2, out):
             )
             v_codes[b], v_scales[b] = vc, vs
 
-        def spread_k2(b):
-            kb = psum.tile([P, N], BF16, tag="gateT1")
-            nc.tensor.matmul(
-                out=kb[:],
-                lhsT=ident_bf16[:, b : b + 1].to_broadcast([P, P]),
-                rhs=k2_rows[:],
-                start=True,
-                stop=True,
-            )
-            k2_spread[b] = kb
-
-        def keep_k2(b):
-            kk = work.tile([P, N], BF16, bufs=3)
-            nc.scalar.copy(out=kk[:], in_=k2_spread[b][:])
-            k2_kept[b] = kk
-
         def gate_rows(b, h):
             if h == 0:
                 ga = work.tile([P, TILES, N], BF16)
@@ -238,7 +231,7 @@ def tile_cross_module_pa_t_kernel(tc, x1, wq1, bq1, wv1, bv1, k2, out):
             for t in (2 * h, 2 * h + 1):
                 nc.scalar.activation(
                     out=gate[b][:, t, :].rearrange("p (u q e) -> p u q e", u=2, e=2),
-                    in_=k2_kept[b][:].rearrange("p (u e q) -> p u q e", u=2, e=2),
+                    in_=k2_all[:, b, :].rearrange("p (u e q) -> p u q e", u=2, e=2),
                     func=ACT.Sigmoid,
                     scale=neg_q1[b][:, t : t + 1],
                 )
@@ -314,7 +307,6 @@ def tile_cross_module_pa_t_kernel(tc, x1, wq1, bq1, wv1, bv1, k2, out):
             when(s + 2, quantise_x)
             when(s, gate_rows, 0)
             when(s, transpose_gate, 0)
-            when(s + 1, keep_k2)
             when(s + 1, transpose_q)
             when(s, gate_rows, 1)
             when(s, transpose_gate, 1)
@@ -329,5 +321,4 @@ def tile_cross_module_pa_t_kernel(tc, x1, wq1, bq1, wv1, bv1, k2, out):
             when(s + 2, project_v, 0)
             when(s + 2, project_q, 0)
             when(s + 2, project_v, 1)
-            when(s + 2, spread_k2)
             when(s + 3, regroup_x)

@@ -301,24 +301,24 @@ def tile_cross_module_pa_t_kernel(tc, x1, wq1, bq1, wv1, bv1, k2, out):
         for s in range(-2, B + 1):
             when(s - 1, quantise_gate)
             when(s - 1, multiply)
-            when(s + 1, bias_q_hi)
-            when(s + 1, max_of_halves)
             when(s, quantise_v)
             when(s + 2, quantise_x)
+            when(s + 1, bias_q_hi)
+            when(s + 1, max_of_halves)
             when(s, gate_rows, 0)
             when(s, transpose_gate, 0)
             when(s + 1, transpose_q)
             when(s, gate_rows, 1)
             when(s, transpose_gate, 1)
             when(s + 1, bias_v, 0)
-            when(s + 1, max_over_channels)
             when(s + 1, bias_v, 1)
+            when(s + 1, max_over_channels)
             when(s, regroup_gate, 0)
             when(s - 1, store, 0)
             when(s, regroup_gate, 1)
             when(s - 1, store, 1)
             when(s + 2, project_q, 1)
             when(s + 2, project_v, 0)
-            when(s + 2, project_q, 0)
             when(s + 2, project_v, 1)
+            when(s + 2, project_q, 0)
             when(s + 3, regroup_x)

@@ -301,8 +301,8 @@ def tile_cross_module_pa_t_kernel(tc, x1, wq1, bq1, wv1, bv1, k2, out):
         for s in range(-2, B + 1):
             when(s - 1, quantise_gate)
             when(s - 1, multiply)
-            when(s, quantise_v)
             when(s + 2, quantise_x)
+            when(s, quantise_v)
             when(s + 1, bias_q_hi)
             when(s + 1, max_of_halves)
             when(s, gate_rows, 0)

@@ -21,7 +21,7 @@ PACK = 4
 TILES = N // P
 HALVES = C2 // P
 WORDS = C // 2
-VECTOR_REGROUPS = 2
+SPREAD = 3
 
 FLOPS = 2 * B * (2 * C2 * C * N + C2 * N * N)
 
@@ -34,12 +34,11 @@ def tile_cross_module_pa_t_kernel(tc, x1, wq1, bq1, wv1, bv1, k2, out):
         xin = stack.enter_context(tc.tile_pool(name="xin", bufs=B))
         work = stack.enter_context(tc.tile_pool(name="work", bufs=2))
 
-        w_rows = const.tile([P, 2 * HALVES, C], BF16)
-        nc.sync.dma_start(out=w_rows[:, 0:HALVES, :], in_=wq1.rearrange("(g o) c -> o g c", o=P))
-        nc.sync.dma_start(out=w_rows[:, HALVES:, :], in_=wv1.rearrange("(g o) c -> o g c", o=P))
-
         bias_rows = const.tile([P, P], BF16)
         nc.vector.memset(bias_rows[:], 0.0)
+        spread_rows = const.tile([P, SPREAD, N], BF16)
+        nc.vector.memset(spread_rows[:], 0.0)
+        w_rows = const.tile([P, 2 * HALVES, C], BF16)
         bv_all = const.tile([P, C2], BF16)
         k2_all = const.tile([P, B, N], BF16)
         x_raw = {}
@@ -58,11 +57,13 @@ def tile_cross_module_pa_t_kernel(tc, x1, wq1, bq1, wv1, bv1, k2, out):
                 in_=k2[first:last].rearrange("b n -> (b n)").partition_broadcast(P),
             )
 
-        nc.sync.dma_start(out=bias_rows[0:HALVES, :], in_=bq1.rearrange("(g o) -> g o", o=P))
+        nc.sync.dma_start(out=w_rows[:, 0:HALVES, :], in_=wq1.rearrange("(g o) c -> o g c", o=P))
         load_x(0)
-        nc.sync.dma_start(out=bv_all[:], in_=bv1.partition_broadcast(P))
+        nc.sync.dma_start(out=bias_rows[0:HALVES, :], in_=bq1.rearrange("(g o) -> g o", o=P))
+        nc.sync.dma_start(out=spread_rows[0:1, 0:2, :], in_=k2[0:2].unsqueeze(0))
+        nc.sync.dma_start(out=spread_rows[0:1, 2, 0:C2], in_=bv1.unsqueeze(0))
+        nc.sync.dma_start(out=w_rows[:, HALVES:, :], in_=wv1.rearrange("(g o) c -> o g c", o=P))
         load_x(1)
-        load_k2(0, 2)
         load_x(2)
         load_k2(2, 4)
         load_x(3)
@@ -79,33 +80,55 @@ def tile_cross_module_pa_t_kernel(tc, x1, wq1, bq1, wv1, bv1, k2, out):
         nc.vector.memset(warm[:], 0.0)
         nc.scalar.activation(out=warm[:], in_=warm[:], func=ACT.Sigmoid)
 
+
+        ones = const.tile([P, P], BF16)
+        nc.vector.memset(ones[:], 1.0)
+
         w_grouped = const.tile([P, 2 * C2 * PACK], BF16, align_bytes=64)
         w_codes = const.tile([P, 2 * C2], U32, align_bytes=64)
         w_scales = const.tile([P, 2 * C2], U8, align_bytes=64)
         bq_cols = const.tile([P, HALVES], F32)
 
-        def transpose_weights():
+        psum = stack.enter_context(tc.psum_pool(name="psum", bufs=1))
+
+        def transpose_weights(i):
             w_words = w_rows[:].rearrange("o g c -> o (g c)").bitcast(F32)
             grouped_words = w_grouped[:].bitcast(F32).rearrange("p (col u) -> p col u", u=2)
-            with tc.psum_pool(name="setup_psum", bufs=1) as setup_psum:
-                for i in range(2):
-                    wT = setup_psum.tile([P, 2, C2], F32, name="wT%d" % i)
-                    for g in range(HALVES):
-                        for u in range(2):
-                            first = (i * HALVES + g) * WORDS + u * P
-                            nc.tensor.transpose(
-                                wT[:, u, g * P : (g + 1) * P],
-                                w_words[:, first : first + P],
-                                ident_f32[:],
-                            )
-                    nc.scalar.copy(
-                        out=grouped_words[:, i * C2 : (i + 1) * C2, :],
-                        in_=wT[:].rearrange("p u col -> p col u"),
+            wT = psum.tile([P, 2, C2], F32, tag="gateT%d" % i, name="wT%d" % i)
+            for g in range(HALVES):
+                for u in range(2):
+                    first = (i * HALVES + g) * WORDS + u * P
+                    nc.tensor.transpose(
+                        wT[:, u, g * P : (g + 1) * P], w_words[:, first : first + P], ident_f32[:]
                     )
-                bqT = setup_psum.tile([P, P], BF16)
-                nc.tensor.transpose(bqT[:], bias_rows[:], ident_bf16[:])
-                nc.scalar.copy(out=bq_cols[:], in_=bqT[:, 0:HALVES])
+            nc.scalar.copy(
+                out=grouped_words[:, i * C2 : (i + 1) * C2, :],
+                in_=wT[:].rearrange("p u col -> p col u"),
+            )
 
+        def quantise_weights(i):
+            cols = slice(i * C2, (i + 1) * C2)
+            nc.vector.quantize_mx(
+                out=w_codes[:, cols].bitcast(FP8X4),
+                scales=w_scales[:, cols],
+                in_=w_grouped[:, i * C2 * PACK : (i + 1) * C2 * PACK],
+            )
+
+        def transpose_bq():
+            bqT = psum.tile([P, P], BF16, tag="out0")
+            nc.tensor.transpose(bqT[:], bias_rows[:], ident_bf16[:])
+            nc.scalar.copy(out=bq_cols[:], in_=bqT[:, 0:HALVES])
+
+        def spread(row, width, tag, to):
+            sp = psum.tile([P, width], BF16, tag=tag, name="spread%d" % row)
+            nc.tensor.matmul(
+                out=sp[:], lhsT=ones[:], rhs=spread_rows[:, row, 0:width], start=True, stop=True
+            )
+            nc.scalar.copy(out=to, in_=sp[:])
+
+        x_buffers = [
+            const.tile([P, N, PACK], BF16, align_bytes=64, name="x_buffer%d" % i) for i in range(2)
+        ]
         x_grouped, x_codes, x_scales = {}, {}, {}
         q_lo, q_hi, q_hi_biased, q_max, q_maxT, neg_q1 = {}, {}, {}, {}, {}, {}
         vT, v_grouped, v_codes, v_scales = {}, {}, {}, {}
@@ -113,8 +136,8 @@ def tile_cross_module_pa_t_kernel(tc, x1, wq1, bq1, wv1, bv1, k2, out):
         product = {}
 
         def regroup_x(b):
-            xg = work.tile([P, N, PACK], BF16, align_bytes=64)
-            if b < VECTOR_REGROUPS:
+            xg = x_buffers[max(b, 1) % 2]
+            if b == 0:
                 nc.vector.tensor_copy(
                     out=xg[:].rearrange("p (c i) t -> p c t i", i=4),
                     in_=x_raw[b][:].rearrange("p t (c i) -> p c t i", i=4),
@@ -247,78 +270,155 @@ def tile_cross_module_pa_t_kernel(tc, x1, wq1, bq1, wv1, bv1, k2, out):
                     )
             gateT[b, h] = gT
 
-        def regroup_gate(b, h):
-            if h == 0:
+        def copy_on(engine, **operands):
+            if engine == "scalar":
+                nc.scalar.copy(**operands)
+            else:
+                nc.vector.tensor_copy(**operands)
+
+        def regroup_gate(b, engine, first, last):
+            if b not in gate_grouped:
                 gg = work.tile([P, N * PACK], BF16, align_bytes=64)
                 gate_grouped[b] = gg
             words = gate_grouped[b][:].bitcast(F32).rearrange("p (m u) -> p m u", u=2)
-            nc.scalar.copy(
-                out=words[:, h * 2 * P : (h + 1) * 2 * P, :],
-                in_=gateT[b, h][:].rearrange("p u m -> p m u"),
+            h = first // (2 * P)
+            bank = slice(first - h * 2 * P, last - h * 2 * P)
+            copy_on(
+                engine,
+                out=words[:, first:last, :],
+                in_=gateT[b, h][:, :, bank].rearrange("p u m -> p m u"),
             )
 
-        def quantise_gate(b):
-            gc = work.tile([P, N], U32, align_bytes=64)
-            gs = work.tile([P, N], U8, align_bytes=64)
-            nc.vector.quantize_mx(out=gc[:].bitcast(FP8X4), scales=gs[:], in_=gate_grouped[b][:])
-            gate_codes[b], gate_scales[b] = gc, gs
+        def quantise_gate(b, first=0, last=N):
+            if first == 0:
+                gc = work.tile([P, N], U32, align_bytes=64)
+                gs = work.tile([P, N], U8, align_bytes=64)
+                gate_codes[b], gate_scales[b] = gc, gs
+            nc.vector.quantize_mx(
+                out=gate_codes[b][:, first:last].bitcast(FP8X4),
+                scales=gate_scales[b][:, first:last],
+                in_=gate_grouped[b][:, first * PACK : last * PACK],
+            )
 
-        def multiply(b):
+        def multiply(b, first=0, last=N):
             for g in range(HALVES):
-                acc = psum.tile([P, N], F32, tag="out%d" % g, name="out%d" % g)
+                if first == 0:
+                    tag = ("vT%d" if b == B - 1 else "out%d") % g
+                    acc = psum.tile([P, N], F32, tag=tag, name="product%d" % g)
+                    product[b, g] = acc
                 cols = slice(g * P, (g + 1) * P)
                 nc.tensor.matmul_mx(
-                    out=acc[:],
+                    out=product[b, g][:, first:last],
                     lhsT=v_codes[b][:, cols].bitcast(FP8X4),
                     lhsT_scale=v_scales[b][:, cols],
-                    rhs=gate_codes[b][:].bitcast(FP8X4),
-                    rhs_scale=gate_scales[b][:],
+                    rhs=gate_codes[b][:, first:last].bitcast(FP8X4),
+                    rhs_scale=gate_scales[b][:, first:last],
                     start=True,
                     stop=True,
                 )
-                product[b, g] = acc
 
-        def store(b, g):
+        def store(b, g, engine, first=0, last=N):
             res = work.tile([P, N], F32, bufs=8)
-            if g == 0:
-                nc.scalar.copy(out=res[:], in_=product[b, g][:])
-            else:
-                nc.vector.tensor_copy(out=res[:], in_=product[b, g][:])
+            copy_on(engine, out=res[:, first:last], in_=product[b, g][:, first:last])
             nc.sync.dma_start(
-                out=out[b, g * P : (g + 1) * P].rearrange("c h w -> c (h w)"), in_=res[:]
+                out=out[b, g * P : (g + 1) * P].rearrange("c h w -> c (h w)")[:, first:last],
+                in_=res[:, first:last],
             )
 
-        regroup_x(0)
-        transpose_weights()
-        nc.vector.quantize_mx(out=w_codes[:].bitcast(FP8X4), scales=w_scales[:], in_=w_grouped[:])
+        def project(b):
+            project_q(b, 1)
+            project_v(b, 0)
+            project_v(b, 1)
+            project_q(b, 0)
 
-        psum = stack.enter_context(tc.psum_pool(name="psum", bufs=1))
+        regroup_x(0)
+        transpose_weights(0)
+        quantise_weights(0)
+        transpose_bq()
+        quantise_x(0)
+        transpose_weights(1)
+        quantise_weights(1)
+        project_q(0, 1)
+        project_q(0, 0)
+        bias_q_hi(0)
+        spread(0, N, "gateT0", k2_all[:, 0, :])
+        spread(2, C2, "out1", bv_all[:])
+        project_v(0, 0)
+        max_of_halves(0)
+        transpose_q(0)
+        project_v(0, 1)
+        regroup_x(1)
+        bias_v(0, 0)
+        max_over_channels(0)
+        gate_rows(0, 0)
+        quantise_x(1)
+        spread(1, N, "out1", k2_all[:, 1, :])
+        bias_v(0, 1)
+        project_q(1, 1)
+        project_q(1, 0)
+        project_v(1, 0)
+        project_v(1, 1)
+        regroup_x(2)
+        bias_q_hi(1)
 
         def when(b, stage, *args):
             if 0 <= b < B:
                 stage(b, *args)
 
-        for s in range(-2, B + 1):
+        for s in range(B - 2):
             when(s - 1, quantise_gate)
             when(s - 1, multiply)
-            when(s + 2, quantise_x)
-            when(s, quantise_v)
-            when(s + 1, bias_q_hi)
-            when(s + 1, max_of_halves)
-            when(s, gate_rows, 0)
-            when(s, transpose_gate, 0)
-            when(s + 1, transpose_q)
-            when(s, gate_rows, 1)
-            when(s, transpose_gate, 1)
-            when(s + 1, bias_v, 0)
-            when(s + 1, bias_v, 1)
-            when(s + 1, max_over_channels)
-            when(s, regroup_gate, 0)
-            when(s - 1, store, 0)
-            when(s, regroup_gate, 1)
-            when(s - 1, store, 1)
-            when(s + 2, project_q, 1)
-            when(s + 2, project_v, 0)
-            when(s + 2, project_v, 1)
-            when(s + 2, project_q, 0)
+            quantise_x(s + 2)
+            quantise_v(s)
+            max_of_halves(s + 1)
+            transpose_gate(s, 0)
+            transpose_q(s + 1)
+            gate_rows(s, 1)
+            transpose_gate(s, 1)
+            bias_v(s + 1, 0)
+            bias_v(s + 1, 1)
+            max_over_channels(s + 1)
+            regroup_gate(s, "scalar", 0, N // 2)
+            when(s - 1, store, 0, "scalar")
+            regroup_gate(s, "scalar", N // 2, N)
+            when(s - 1, store, 1, "vector")
+            project(s + 2)
+            bias_q_hi(s + 2)
+            gate_rows(s + 1, 0)
             when(s + 3, regroup_x)
+
+        last = B - 1
+        quantise_gate(last - 2)
+        multiply(last - 2)
+        quantise_v(last - 1)
+        max_of_halves(last)
+        transpose_gate(last - 1, 0)
+        transpose_q(last)
+        gate_rows(last - 1, 1)
+        transpose_gate(last - 1, 1)
+        store(last - 2, 0, "vector")
+        max_over_channels(last)
+        store(last - 2, 1, "vector")
+        regroup_gate(last - 1, "scalar", 0, N // 2)
+        regroup_gate(last - 1, "scalar", N // 2, N)
+        gate_rows(last, 0)
+        transpose_gate(last, 0)
+        quantise_gate(last - 1)
+        multiply(last - 1)
+        bias_v(last, 0)
+        bias_v(last, 1)
+        gate_rows(last, 1)
+        transpose_gate(last, 1)
+        quantise_v(last)
+        regroup_gate(last, "vector", N // 2, N // 2 + P)
+        regroup_gate(last, "scalar", 0, N // 2)
+        regroup_gate(last, "scalar", N // 2 + P, N)
+        quantise_gate(last, 0, N // 2)
+        multiply(last, 0, N // 2)
+        quantise_gate(last, N // 2, N)
+        multiply(last, N // 2, N)
+        store(last - 1, 0, "scalar")
+        store(last - 1, 1, "vector")
+        for first in (0, N // 2):
+            store(last, 0, "scalar", first, first + N // 2)
+            store(last, 1, "vector", first, first + N // 2)

@@ -21,6 +21,7 @@ PACK = 4
 TILES = N // P
 HALVES = C2 // P
 WORDS = C // 2
+WHOLE, LEFT, RIGHT = slice(0, N), slice(0, N // 2), slice(N // 2, N)
 SPREAD = 3
 
 FLOPS = 2 * B * (2 * C2 * C * N + C2 * N * N)
@@ -45,10 +46,15 @@ def tile_cross_module_pa_t_kernel(tc, x1, wq1, bq1, wv1, bv1, k2, out):
 
         def load_x(b):
             xr = xin.tile([P, PACK, N], BF16)
-            nc.sync.dma_start(
-                out=xr[:].rearrange("p (u e) n -> p u e n", u=2),
-                in_=x1[b].rearrange("(u p e) h w -> p u e (h w)", u=2, e=2),
-            )
+            rows = x1[b].rearrange("(u p e) h w -> p u e (h w)", u=2, e=2)
+            if b == 0:
+                for part in (LEFT, RIGHT):
+                    for u in range(2):
+                        nc.sync.dma_start(
+                            out=xr[:, 2 * u : 2 * u + 2, part], in_=rows[:, u, :, part]
+                        )
+            else:
+                nc.sync.dma_start(out=xr[:].rearrange("p (u e) n -> p u e n", u=2), in_=rows)
             x_raw[b] = xr
 
         def load_k2(first, last):
@@ -59,10 +65,10 @@ def tile_cross_module_pa_t_kernel(tc, x1, wq1, bq1, wv1, bv1, k2, out):
 
         nc.sync.dma_start(out=w_rows[:, 0:HALVES, :], in_=wq1.rearrange("(g o) c -> o g c", o=P))
         load_x(0)
+        nc.sync.dma_start(out=w_rows[:, HALVES:, :], in_=wv1.rearrange("(g o) c -> o g c", o=P))
         nc.sync.dma_start(out=bias_rows[0:HALVES, :], in_=bq1.rearrange("(g o) -> g o", o=P))
         nc.sync.dma_start(out=spread_rows[0:1, 0:2, :], in_=k2[0:2].unsqueeze(0))
         nc.sync.dma_start(out=spread_rows[0:1, 2, 0:C2], in_=bv1.unsqueeze(0))
-        nc.sync.dma_start(out=w_rows[:, HALVES:, :], in_=wv1.rearrange("(g o) c -> o g c", o=P))
         load_x(1)
         load_x(2)
         load_k2(2, 4)
@@ -129,39 +135,39 @@ def tile_cross_module_pa_t_kernel(tc, x1, wq1, bq1, wv1, bv1, k2, out):
         x_buffers = [
             const.tile([P, N, PACK], BF16, align_bytes=64, name="x_buffer%d" % i) for i in range(2)
         ]
-        x_grouped, x_codes, x_scales = {}, {}, {}
-        q_lo, q_hi, q_hi_biased, q_max, q_maxT, neg_q1 = {}, {}, {}, {}, {}, {}
+        x_codes, x_scales = {}, {}
+        q, q_hi_biased, q_max, q_maxT, neg_q1 = {}, {}, {}, {}, {}
         vT, v_grouped, v_codes, v_scales = {}, {}, {}, {}
         gate, gateT, gate_grouped, gate_codes, gate_scales = {}, {}, {}, {}, {}
         product = {}
 
-        def regroup_x(b):
-            xg = x_buffers[max(b, 1) % 2]
+        def regroup_x(b, part=WHOLE):
+            xg = x_buffers[max(b, 1) % 2][:, part, :]
             if b == 0:
                 nc.vector.tensor_copy(
-                    out=xg[:].rearrange("p (c i) t -> p c t i", i=4),
-                    in_=x_raw[b][:].rearrange("p t (c i) -> p c t i", i=4),
+                    out=xg.rearrange("p (c i) t -> p c t i", i=4),
+                    in_=x_raw[b][:, :, part].rearrange("p t (c i) -> p c t i", i=4),
                 )
             else:
                 nc.gpsimd.tensor_scalar(
-                    out=xg[:],
+                    out=xg,
                     in0=x_raw[b][:].rearrange("p t n -> p n t"),
                     scalar1=1.0,
                     scalar2=0.0,
                     op0=ALU.mult,
                     op1=ALU.add,
                 )
-            x_grouped[b] = xg
 
-        def quantise_x(b):
-            xc = work.tile([P, N], U32, align_bytes=64)
-            xs = work.tile([P, N], U8, align_bytes=64)
+        def quantise_x(b, part=WHOLE):
+            if b not in x_codes:
+                xc = work.tile([P, N], U32, align_bytes=64)
+                xs = work.tile([P, N], U8, align_bytes=64)
+                x_codes[b], x_scales[b] = xc, xs
             nc.vector.quantize_mx(
-                out=xc[:].bitcast(FP8X4),
-                scales=xs[:],
-                in_=x_grouped[b][:].rearrange("p n t -> p (n t)"),
+                out=x_codes[b][:, part].bitcast(FP8X4),
+                scales=x_scales[b][:, part],
+                in_=x_buffers[max(b, 1) % 2][:, part, :].rearrange("p n t -> p (n t)"),
             )
-            x_codes[b], x_scales[b] = xc, xs
 
         def project_v(b, h):
             acc = psum.tile([P, TILES, P], F32, tag="vT%d" % h, name="vT%d" % h)
@@ -179,51 +185,64 @@ def tile_cross_module_pa_t_kernel(tc, x1, wq1, bq1, wv1, bv1, k2, out):
                 )
             vT[b, h] = acc
 
-        def project_q(b, g):
-            acc = psum.tile([P, N], F32, tag=("q_lo", "q_hi")[g], name="q%d" % g)
+        def q_tag(part, g):
+            return ("out%d" if part == RIGHT else "q%d") % g
+
+        def project_q(b, g, part=WHOLE):
+            acc = psum.tile([P, N], F32, tag=q_tag(part, g), name="q%d" % g)
             cols = slice(g * P, (g + 1) * P)
             nc.tensor.matmul_mx(
-                out=acc[:],
+                out=acc[:, part],
                 lhsT=w_codes[:, cols].bitcast(FP8X4),
                 lhsT_scale=w_scales[:, cols],
-                rhs=x_codes[b][:].bitcast(FP8X4),
-                rhs_scale=x_scales[b][:],
+                rhs=x_codes[b][:, part].bitcast(FP8X4),
+                rhs_scale=x_scales[b][:, part],
                 start=True,
                 stop=True,
             )
-            (q_lo, q_hi)[g][b] = acc
+            q[b, g] = acc
 
-        def bias_q_hi(b):
+        def bias_q_hi(b, part=WHOLE):
             qb = work.tile([P, N], F32)
             nc.scalar.activation(
-                out=qb[:], in_=q_hi[b][:], func=ACT.Identity, bias=bq_cols[:, 1:2], scale=1.0
+                out=qb[:, part],
+                in_=q[b, 1][:, part],
+                func=ACT.Identity,
+                bias=bq_cols[:, 1:2],
+                scale=1.0,
             )
             q_hi_biased[b] = qb
 
-        def max_of_halves(b):
+        def max_of_halves(b, part=WHOLE):
             qm = work.tile([P, N], F32)
             nc.vector.scalar_tensor_tensor(
-                out=qm[:],
-                in0=q_lo[b][:],
+                out=qm[:, part],
+                in0=q[b, 0][:, part],
                 scalar=bq_cols[:, 0:1],
-                in1=q_hi_biased[b][:],
+                in1=q_hi_biased[b][:, part],
                 op0=ALU.add,
                 op1=ALU.max,
             )
             q_max[b] = qm
 
-        def transpose_q(b):
-            qT = psum.tile([P, TILES, P], F32, tag="q_lo")
-            for t in range(TILES):
+        def transpose_q(b, part=WHOLE):
+            qT = psum.tile([P, TILES, P], F32, tag=q_tag(part, 0))
+            for t in range(part.start // P, part.stop // P):
                 nc.tensor.transpose(qT[:, t, :], q_max[b][:, t * P : (t + 1) * P], ident_f32[:])
-            q_maxT[b] = qT
+            q_maxT[b, part.start] = qT
 
-        def max_over_channels(b):
-            nq = work.tile([P, TILES], F32, bufs=3)
+        def max_over_channels(b, part=WHOLE):
+            if b not in neg_q1:
+                nq = work.tile([P, TILES], F32, bufs=3)
+                neg_q1[b] = nq
+            tiles = slice(part.start // P, part.stop // P)
             nc.vector.tensor_reduce(
-                out=nq[:], in_=q_maxT[b][:], axis=AXIS.X, op=ALU.max, negate=True
+                out=neg_q1[b][:, tiles],
+                in_=q_maxT[b, part.start][:, tiles, :],
+                axis=AXIS.X,
+                op=ALU.max,
+                negate=True,
             )
-            neg_q1[b] = nq
 
         def bias_v(b, h):
             if h == 0:
@@ -259,16 +278,16 @@ def tile_cross_module_pa_t_kernel(tc, x1, wq1, bq1, wv1, bv1, k2, out):
                     scale=neg_q1[b][:, t : t + 1],
                 )
 
-        def transpose_gate(b, h):
+        def transpose_gate(b, tag, *tiles):
             words = gate[b][:].rearrange("p t k -> p (t k)").bitcast(F32)
-            gT = psum.tile([P, 2, 2 * P], F32, tag="gateT%d" % h, name="gateT%d" % h)
-            for j in range(2):
+            gT = psum.tile([P, 2, 2 * P], F32, tag=tag, name="gateT_" + tag)
+            for j, t in enumerate(tiles):
                 for u in range(2):
-                    first = (2 * h + j) * WORDS + u * P
+                    first = t * WORDS + u * P
                     nc.tensor.transpose(
                         gT[:, u, j * P : (j + 1) * P], words[:, first : first + P], ident_f32[:]
                     )
-            gateT[b, h] = gT
+            gateT[b, tiles] = gT
 
         def copy_on(engine, **operands):
             if engine == "scalar":
@@ -276,17 +295,15 @@ def tile_cross_module_pa_t_kernel(tc, x1, wq1, bq1, wv1, bv1, k2, out):
             else:
                 nc.vector.tensor_copy(**operands)
 
-        def regroup_gate(b, engine, first, last):
+        def regroup_gate(b, engine, *tiles):
             if b not in gate_grouped:
                 gg = work.tile([P, N * PACK], BF16, align_bytes=64)
                 gate_grouped[b] = gg
             words = gate_grouped[b][:].bitcast(F32).rearrange("p (m u) -> p m u", u=2)
-            h = first // (2 * P)
-            bank = slice(first - h * 2 * P, last - h * 2 * P)
             copy_on(
                 engine,
-                out=words[:, first:last, :],
-                in_=gateT[b, h][:, :, bank].rearrange("p u m -> p m u"),
+                out=words[:, tiles[0] * P : (tiles[-1] + 1) * P, :],
+                in_=gateT[b, tiles][:, :, 0 : len(tiles) * P].rearrange("p u m -> p m u"),
             )
 
         def quantise_gate(b, first=0, last=N):
@@ -331,94 +348,118 @@ def tile_cross_module_pa_t_kernel(tc, x1, wq1, bq1, wv1, bv1, k2, out):
             project_v(b, 1)
             project_q(b, 0)
 
-        regroup_x(0)
+        regroup_x(0, LEFT)
         transpose_weights(0)
+        regroup_x(0, RIGHT)
         quantise_weights(0)
         transpose_bq()
-        quantise_x(0)
+        quantise_x(0, LEFT)
+        quantise_x(0, RIGHT)
         transpose_weights(1)
-        quantise_weights(1)
-        project_q(0, 1)
-        project_q(0, 0)
-        bias_q_hi(0)
+        project_q(0, 1, LEFT)
+        bias_q_hi(0, LEFT)
+        project_q(0, 0, LEFT)
+        max_of_halves(0, LEFT)
+        project_q(0, 1, RIGHT)
+        bias_q_hi(0, RIGHT)
+        project_q(0, 0, RIGHT)
         spread(0, N, "gateT0", k2_all[:, 0, :])
-        spread(2, C2, "out1", bv_all[:])
-        project_v(0, 0)
-        max_of_halves(0)
-        transpose_q(0)
-        project_v(0, 1)
-        regroup_x(1)
-        bias_v(0, 0)
-        max_over_channels(0)
+        transpose_q(0, LEFT)
+        max_of_halves(0, RIGHT)
+        transpose_q(0, RIGHT)
+        max_over_channels(0, LEFT)
         gate_rows(0, 0)
+        max_over_channels(0, RIGHT)
+        spread(2, C2, "out1", bv_all[:])
+        gate_rows(0, 1)
+        quantise_weights(1)
+        project_v(0, 0)
+        regroup_x(1)
         quantise_x(1)
-        spread(1, N, "out1", k2_all[:, 1, :])
-        bias_v(0, 1)
         project_q(1, 1)
         project_q(1, 0)
+        project_v(0, 1)
+        bias_q_hi(1)
+        bias_v(0, 0)
+        bias_v(0, 1)
+        spread(1, N, "out1", k2_all[:, 1, :])
+        regroup_x(2)
+
+        transpose_gate(0, "gateT0", 0, 1)
+        transpose_gate(0, "gateT1", 2, 3)
+        max_of_halves(1)
         project_v(1, 0)
         project_v(1, 1)
-        regroup_x(2)
-        bias_q_hi(1)
+        transpose_q(1)
+        quantise_x(2)
+        max_over_channels(1)
+        regroup_gate(0, "scalar", 0, 1)
+        regroup_gate(0, "scalar", 2, 3)
+        quantise_v(0)
+        bias_v(1, 0)
+        bias_v(1, 1)
+        project(2)
+        bias_q_hi(2)
+        gate_rows(1, 0)
+        gate_rows(1, 1)
+        regroup_x(3)
 
-        def when(b, stage, *args):
-            if 0 <= b < B:
-                stage(b, *args)
-
-        for s in range(B - 2):
-            when(s - 1, quantise_gate)
-            when(s - 1, multiply)
+        for s in range(1, B - 2):
+            quantise_gate(s - 1)
+            multiply(s - 1)
             quantise_x(s + 2)
             quantise_v(s)
             max_of_halves(s + 1)
-            transpose_gate(s, 0)
+            transpose_gate(s, "gateT0", 0, 1)
             transpose_q(s + 1)
-            gate_rows(s, 1)
-            transpose_gate(s, 1)
+            transpose_gate(s, "gateT1", 2, 3)
             bias_v(s + 1, 0)
             bias_v(s + 1, 1)
             max_over_channels(s + 1)
-            regroup_gate(s, "scalar", 0, N // 2)
-            when(s - 1, store, 0, "scalar")
-            regroup_gate(s, "scalar", N // 2, N)
-            when(s - 1, store, 1, "vector")
+            regroup_gate(s, "scalar", 0, 1)
+            store(s - 1, 0, "scalar")
+            regroup_gate(s, "scalar", 2, 3)
+            store(s - 1, 1, "vector")
             project(s + 2)
             bias_q_hi(s + 2)
             gate_rows(s + 1, 0)
-            when(s + 3, regroup_x)
+            gate_rows(s + 1, 1)
+            if s + 3 < B:
+                regroup_x(s + 3)
 
         last = B - 1
         quantise_gate(last - 2)
         multiply(last - 2)
         quantise_v(last - 1)
         max_of_halves(last)
-        transpose_gate(last - 1, 0)
+        transpose_gate(last - 1, "gateT0", 0, 1)
         transpose_q(last)
-        gate_rows(last - 1, 1)
-        transpose_gate(last - 1, 1)
+        transpose_gate(last - 1, "gateT1", 2, 3)
         store(last - 2, 0, "vector")
         max_over_channels(last)
         store(last - 2, 1, "vector")
-        regroup_gate(last - 1, "scalar", 0, N // 2)
-        regroup_gate(last - 1, "scalar", N // 2, N)
+        regroup_gate(last - 1, "scalar", 0, 1)
+        regroup_gate(last - 1, "scalar", 2, 3)
         gate_rows(last, 0)
-        transpose_gate(last, 0)
+        transpose_gate(last, "gateT0", 0, 1)
         quantise_gate(last - 1)
         multiply(last - 1)
         bias_v(last, 0)
         bias_v(last, 1)
-        gate_rows(last, 1)
-        transpose_gate(last, 1)
         quantise_v(last)
-        regroup_gate(last, "vector", N // 2, N // 2 + P)
-        regroup_gate(last, "scalar", 0, N // 2)
-        regroup_gate(last, "scalar", N // 2 + P, N)
+        gate_rows(last, 1)
+        transpose_gate(last, "gateT1", 2)
+        transpose_gate(last, "q0", 3)
+        regroup_gate(last, "scalar", 0, 1)
+        store(last - 1, 0, "scalar")
+        regroup_gate(last, "vector", 2)
+        regroup_gate(last, "scalar", 3)
         quantise_gate(last, 0, N // 2)
         multiply(last, 0, N // 2)
         quantise_gate(last, N // 2, N)
+        store(last - 1, 1, "scalar")
+        store(last, 1, "vector", 0, N // 2)
+        store(last, 0, "scalar", 0, N // 2)
         multiply(last, N // 2, N)
-        store(last - 1, 0, "scalar")
-        store(last - 1, 1, "vector")
-        for first in (0, N // 2):
-            store(last, 0, "scalar", first, first + N // 2)
-            store(last, 1, "vector", first, first + N // 2)
+        store(last, 1, "vector", N // 2, N)
+        store(last, 0, "scalar", N // 2, N)

@@ -22,6 +22,7 @@ TILES = N // P
 HALVES = C2 // P
 WORDS = C // 2
 WHOLE, LEFT, RIGHT = slice(0, N), slice(0, N // 2), slice(N // 2, N)
+VECTOR_REGROUPS = 4
 SPREAD = 3
 
 FLOPS = 2 * B * (2 * C2 * C * N + C2 * N * N)
@@ -133,7 +134,8 @@ def tile_cross_module_pa_t_kernel(tc, x1, wq1, bq1, wv1, bv1, k2, out):
             nc.scalar.copy(out=to, in_=sp[:])
 
         x_buffers = [
-            const.tile([P, N, PACK], BF16, align_bytes=64, name="x_buffer%d" % i) for i in range(2)
+            const.tile([P, N, PACK], BF16, align_bytes=64, name="x_buffer%d" % i)
+            for i in range(VECTOR_REGROUPS + 1)
         ]
         x_codes, x_scales = {}, {}
         q, q_hi_biased, q_max, q_maxT, neg_q1 = {}, {}, {}, {}, {}
@@ -141,9 +143,12 @@ def tile_cross_module_pa_t_kernel(tc, x1, wq1, bq1, wv1, bv1, k2, out):
         gate, gateT, gate_grouped, gate_codes, gate_scales = {}, {}, {}, {}, {}
         product = {}
 
+        def x_buffer(b):
+            return x_buffers[min(b, VECTOR_REGROUPS)]
+
         def regroup_x(b, part=WHOLE):
-            xg = x_buffers[max(b, 1) % 2][:, part, :]
-            if b == 0:
+            xg = x_buffer(b)[:, part, :]
+            if b < VECTOR_REGROUPS:
                 nc.vector.tensor_copy(
                     out=xg.rearrange("p (c i) t -> p c t i", i=4),
                     in_=x_raw[b][:, :, part].rearrange("p t (c i) -> p c t i", i=4),
@@ -166,7 +171,7 @@ def tile_cross_module_pa_t_kernel(tc, x1, wq1, bq1, wv1, bv1, k2, out):
             nc.vector.quantize_mx(
                 out=x_codes[b][:, part].bitcast(FP8X4),
                 scales=x_scales[b][:, part],
-                in_=x_buffers[max(b, 1) % 2][:, part, :].rearrange("p n t -> p (n t)"),
+                in_=x_buffer(b)[:, part, :].rearrange("p n t -> p (n t)"),
             )
 
         def project_v(b, h):
@@ -200,35 +205,37 @@ def tile_cross_module_pa_t_kernel(tc, x1, wq1, bq1, wv1, bv1, k2, out):
                 start=True,
                 stop=True,
             )
-            q[b, g] = acc
+            q[b, g, part.start] = acc
 
         def bias_q_hi(b, part=WHOLE):
             qb = work.tile([P, N], F32)
             nc.scalar.activation(
                 out=qb[:, part],
-                in_=q[b, 1][:, part],
+                in_=q[b, 1, part.start][:, part],
                 func=ACT.Identity,
                 bias=bq_cols[:, 1:2],
                 scale=1.0,
             )
-            q_hi_biased[b] = qb
+            q_hi_biased[b, part.start] = qb
 
         def max_of_halves(b, part=WHOLE):
             qm = work.tile([P, N], F32)
             nc.vector.scalar_tensor_tensor(
                 out=qm[:, part],
-                in0=q[b, 0][:, part],
+                in0=q[b, 0, part.start][:, part],
                 scalar=bq_cols[:, 0:1],
-                in1=q_hi_biased[b][:, part],
+                in1=q_hi_biased[b, part.start][:, part],
                 op0=ALU.add,
                 op1=ALU.max,
             )
-            q_max[b] = qm
+            q_max[b, part.start] = qm
 
         def transpose_q(b, part=WHOLE):
             qT = psum.tile([P, TILES, P], F32, tag=q_tag(part, 0))
             for t in range(part.start // P, part.stop // P):
-                nc.tensor.transpose(qT[:, t, :], q_max[b][:, t * P : (t + 1) * P], ident_f32[:])
+                nc.tensor.transpose(
+                    qT[:, t, :], q_max[b, part.start][:, t * P : (t + 1) * P], ident_f32[:]
+                )
             q_maxT[b, part.start] = qT
 
         def max_over_channels(b, part=WHOLE):
@@ -288,6 +295,12 @@ def tile_cross_module_pa_t_kernel(tc, x1, wq1, bq1, wv1, bv1, k2, out):
                         gT[:, u, j * P : (j + 1) * P], words[:, first : first + P], ident_f32[:]
                     )
             gateT[b, tiles] = gT
+
+        def keep_clock(tag):
+            idle = psum.tile([P, N], F32, tag=tag)
+            nc.tensor.matmul(
+                out=idle[:], lhsT=ident_bf16[:], rhs=k2_all[:, 0, :], start=True, stop=True
+            )
 
         def copy_on(engine, **operands):
             if engine == "scalar":
@@ -359,10 +372,11 @@ def tile_cross_module_pa_t_kernel(tc, x1, wq1, bq1, wv1, bv1, k2, out):
         project_q(0, 1, LEFT)
         bias_q_hi(0, LEFT)
         project_q(0, 0, LEFT)
-        max_of_halves(0, LEFT)
         project_q(0, 1, RIGHT)
         bias_q_hi(0, RIGHT)
         project_q(0, 0, RIGHT)
+        regroup_x(1, LEFT)
+        max_of_halves(0, LEFT)
         spread(0, N, "gateT0", k2_all[:, 0, :])
         transpose_q(0, LEFT)
         max_of_halves(0, RIGHT)
@@ -370,41 +384,68 @@ def tile_cross_module_pa_t_kernel(tc, x1, wq1, bq1, wv1, bv1, k2, out):
         max_over_channels(0, LEFT)
         gate_rows(0, 0)
         max_over_channels(0, RIGHT)
+        quantise_weights(1)
         spread(2, C2, "out1", bv_all[:])
         gate_rows(0, 1)
-        quantise_weights(1)
-        project_v(0, 0)
-        regroup_x(1)
+        regroup_x(1, RIGHT)
         quantise_x(1)
+        project_v(0, 0)
+        project_v(0, 1)
+
         project_q(1, 1)
         project_q(1, 0)
-        project_v(0, 1)
-        bias_q_hi(1)
-        bias_v(0, 0)
-        bias_v(0, 1)
-        spread(1, N, "out1", k2_all[:, 1, :])
-        regroup_x(2)
-
         transpose_gate(0, "gateT0", 0, 1)
+        bias_q_hi(1)
+        regroup_gate(0, "scalar", 0, 1)
+        spread(1, N, "out1", k2_all[:, 1, :])
         transpose_gate(0, "gateT1", 2, 3)
+        bias_v(0, 0)
+        regroup_x(2)
         max_of_halves(1)
-        project_v(1, 0)
-        project_v(1, 1)
         transpose_q(1)
+        bias_v(0, 1)
+        regroup_gate(0, "scalar", 2, 3)
+        project_v(1, 0)
         quantise_x(2)
         max_over_channels(1)
-        regroup_gate(0, "scalar", 0, 1)
-        regroup_gate(0, "scalar", 2, 3)
+        project_q(2, 1)
         quantise_v(0)
-        bias_v(1, 0)
-        bias_v(1, 1)
-        project(2)
-        bias_q_hi(2)
+        project_v(1, 1)
+        project_q(2, 0)
         gate_rows(1, 0)
+        bias_q_hi(2)
         gate_rows(1, 1)
-        regroup_x(3)
 
-        for s in range(1, B - 2):
+        quantise_gate(0)
+        multiply(0)
+        regroup_x(3)
+        bias_v(1, 0)
+        transpose_gate(1, "gateT0", 0, 1)
+        max_of_halves(2)
+        transpose_q(2)
+        bias_v(1, 1)
+        quantise_x(3)
+        transpose_gate(1, "gateT1", 2, 3)
+        project_q(3, 1)
+        quantise_v(1)
+        max_over_channels(2)
+        project_v(2, 0)
+        project_v(2, 1)
+        store(0, 1, "vector")
+        regroup_gate(1, "scalar", 0, 1)
+        store(0, 0, "scalar")
+        regroup_gate(1, "scalar", 2, 3)
+        bias_q_hi(3)
+        bias_v(2, 0)
+        bias_v(2, 1)
+        project_q(3, 0)
+        gate_rows(2, 0)
+        gate_rows(2, 1)
+        regroup_x(4)
+        project_v(3, 0)
+        project_v(3, 1)
+
+        for s in range(2, B - 2):
             quantise_gate(s - 1)
             multiply(s - 1)
             quantise_x(s + 2)
@@ -441,6 +482,8 @@ def tile_cross_module_pa_t_kernel(tc, x1, wq1, bq1, wv1, bv1, k2, out):
         regroup_gate(last - 1, "scalar", 0, 1)
         regroup_gate(last - 1, "scalar", 2, 3)
         gate_rows(last, 0)
+        for i in range(3):
+            keep_clock("q1")
         transpose_gate(last, "gateT0", 0, 1)
         quantise_gate(last - 1)
         multiply(last - 1)

@@ -22,7 +22,7 @@ TILES = N // P
 HALVES = C2 // P
 WORDS = C // 2
 WHOLE, LEFT, RIGHT = slice(0, N), slice(0, N // 2), slice(N // 2, N)
-VECTOR_REGROUPS = 4
+FIRST_BATCHES = 4
 SPREAD = 3
 
 FLOPS = 2 * B * (2 * C2 * C * N + C2 * N * N)
@@ -36,10 +36,16 @@ def tile_cross_module_pa_t_kernel(tc, x1, wq1, bq1, wv1, bv1, k2, out):
         xin = stack.enter_context(tc.tile_pool(name="xin", bufs=B))
         work = stack.enter_context(tc.tile_pool(name="work", bufs=2))
 
+        warm = const.tile([P, 1], F32)
+        nc.vector.memset(warm[:], 0.0)
+        nc.scalar.activation(out=warm[:], in_=warm[:], func=ACT.Sigmoid)
+
+        zeros = const.tile([P, N], BF16)
+        nc.vector.memset(zeros[:].bitcast(U32), 0)
         bias_rows = const.tile([P, P], BF16)
-        nc.vector.memset(bias_rows[:], 0.0)
+        nc.vector.memset(bias_rows[:].bitcast(U32), 0)
         spread_rows = const.tile([P, SPREAD, N], BF16)
-        nc.vector.memset(spread_rows[:], 0.0)
+        nc.vector.memset(spread_rows[:].rearrange("p r n -> p (r n)").bitcast(U32), 0)
         w_rows = const.tile([P, 2 * HALVES, C], BF16)
         bv_all = const.tile([P, C2], BF16)
         k2_all = const.tile([P, B, N], BF16)
@@ -83,10 +89,6 @@ def tile_cross_module_pa_t_kernel(tc, x1, wq1, bq1, wv1, bv1, k2, out):
         ident_bf16 = const.tile([P, P], BF16)
         make_identity(nc, ident_bf16[:])
 
-        warm = const.tile([P, 1], F32)
-        nc.vector.memset(warm[:], 0.0)
-        nc.scalar.activation(out=warm[:], in_=warm[:], func=ACT.Sigmoid)
-
 
         ones = const.tile([P, P], BF16)
         nc.vector.memset(ones[:], 1.0)
@@ -97,6 +99,13 @@ def tile_cross_module_pa_t_kernel(tc, x1, wq1, bq1, wv1, bv1, k2, out):
         bq_cols = const.tile([P, HALVES], F32)
 
         psum = stack.enter_context(tc.psum_pool(name="psum", bufs=1))
+
+        def keep_clock(tag, count):
+            for i in range(count):
+                idle = psum.tile([P, N], F32, tag=tag)
+                nc.tensor.matmul(
+                    out=idle[:], lhsT=zeros[:, 0:P], rhs=zeros[:], start=True, stop=True
+                )
 
         def transpose_weights(i):
             w_words = w_rows[:].rearrange("o g c -> o (g c)").bitcast(F32)
@@ -135,7 +144,7 @@ def tile_cross_module_pa_t_kernel(tc, x1, wq1, bq1, wv1, bv1, k2, out):
 
         x_buffers = [
             const.tile([P, N, PACK], BF16, align_bytes=64, name="x_buffer%d" % i)
-            for i in range(VECTOR_REGROUPS + 1)
+            for i in range(FIRST_BATCHES + 1)
         ]
         x_codes, x_scales = {}, {}
         q, q_hi_biased, q_max, q_maxT, neg_q1 = {}, {}, {}, {}, {}
@@ -144,19 +153,22 @@ def tile_cross_module_pa_t_kernel(tc, x1, wq1, bq1, wv1, bv1, k2, out):
         product = {}
 
         def x_buffer(b):
-            return x_buffers[min(b, VECTOR_REGROUPS)]
+            return x_buffers[min(b, FIRST_BATCHES)]
 
-        def regroup_x(b, part=WHOLE):
+        def regroup_x(b, engine, part=WHOLE):
             xg = x_buffer(b)[:, part, :]
-            if b < VECTOR_REGROUPS:
+            xr = x_raw[b][:, :, part]
+            if engine == "vector":
                 nc.vector.tensor_copy(
                     out=xg.rearrange("p (c i) t -> p c t i", i=4),
-                    in_=x_raw[b][:, :, part].rearrange("p t (c i) -> p c t i", i=4),
+                    in_=xr.rearrange("p t (c i) -> p c t i", i=4),
                 )
+            elif engine == "scalar":
+                nc.scalar.copy(out=xg, in_=xr.rearrange("p t n -> p n t"))
             else:
                 nc.gpsimd.tensor_scalar(
                     out=xg,
-                    in0=x_raw[b][:].rearrange("p t n -> p n t"),
+                    in0=xr.rearrange("p t n -> p n t"),
                     scalar1=1.0,
                     scalar2=0.0,
                     op0=ALU.mult,
@@ -296,12 +308,6 @@ def tile_cross_module_pa_t_kernel(tc, x1, wq1, bq1, wv1, bv1, k2, out):
                     )
             gateT[b, tiles] = gT
 
-        def keep_clock(tag):
-            idle = psum.tile([P, N], F32, tag=tag)
-            nc.tensor.matmul(
-                out=idle[:], lhsT=ident_bf16[:], rhs=k2_all[:, 0, :], start=True, stop=True
-            )
-
         def copy_on(engine, **operands):
             if engine == "scalar":
                 nc.scalar.copy(**operands)
@@ -361,9 +367,11 @@ def tile_cross_module_pa_t_kernel(tc, x1, wq1, bq1, wv1, bv1, k2, out):
             project_v(b, 1)
             project_q(b, 0)
 
-        regroup_x(0, LEFT)
+        keep_clock("vT0", 3)
+        regroup_x(0, "vector", LEFT)
         transpose_weights(0)
-        regroup_x(0, RIGHT)
+        keep_clock("vT0", 2)
+        regroup_x(0, "vector", RIGHT)
         quantise_weights(0)
         transpose_bq()
         quantise_x(0, LEFT)
@@ -375,7 +383,7 @@ def tile_cross_module_pa_t_kernel(tc, x1, wq1, bq1, wv1, bv1, k2, out):
         project_q(0, 1, RIGHT)
         bias_q_hi(0, RIGHT)
         project_q(0, 0, RIGHT)
-        regroup_x(1, LEFT)
+        regroup_x(1, "vector", LEFT)
         max_of_halves(0, LEFT)
         spread(0, N, "gateT0", k2_all[:, 0, :])
         transpose_q(0, LEFT)
@@ -387,7 +395,7 @@ def tile_cross_module_pa_t_kernel(tc, x1, wq1, bq1, wv1, bv1, k2, out):
         quantise_weights(1)
         spread(2, C2, "out1", bv_all[:])
         gate_rows(0, 1)
-        regroup_x(1, RIGHT)
+        regroup_x(1, "vector", RIGHT)
         quantise_x(1)
         project_v(0, 0)
         project_v(0, 1)
@@ -400,11 +408,12 @@ def tile_cross_module_pa_t_kernel(tc, x1, wq1, bq1, wv1, bv1, k2, out):
         spread(1, N, "out1", k2_all[:, 1, :])
         transpose_gate(0, "gateT1", 2, 3)
         bias_v(0, 0)
-        regroup_x(2)
+        regroup_x(2, "vector")
         max_of_halves(1)
         transpose_q(1)
         bias_v(0, 1)
         regroup_gate(0, "scalar", 2, 3)
+        regroup_x(3, "scalar", RIGHT)
         project_v(1, 0)
         quantise_x(2)
         max_over_channels(1)
@@ -418,20 +427,20 @@ def tile_cross_module_pa_t_kernel(tc, x1, wq1, bq1, wv1, bv1, k2, out):
 
         quantise_gate(0)
         multiply(0)
-        regroup_x(3)
+        regroup_x(3, "vector", LEFT)
         bias_v(1, 0)
-        transpose_gate(1, "gateT0", 0, 1)
-        max_of_halves(2)
-        transpose_q(2)
         bias_v(1, 1)
         quantise_x(3)
+        quantise_v(1)
+        transpose_gate(1, "gateT0", 0, 1)
+        max_of_halves(2)
         transpose_gate(1, "gateT1", 2, 3)
         project_q(3, 1)
-        quantise_v(1)
+        transpose_q(2)
+        store(0, 1, "vector")
         max_over_channels(2)
         project_v(2, 0)
         project_v(2, 1)
-        store(0, 1, "vector")
         regroup_gate(1, "scalar", 0, 1)
         store(0, 0, "scalar")
         regroup_gate(1, "scalar", 2, 3)
@@ -441,7 +450,7 @@ def tile_cross_module_pa_t_kernel(tc, x1, wq1, bq1, wv1, bv1, k2, out):
         project_q(3, 0)
         gate_rows(2, 0)
         gate_rows(2, 1)
-        regroup_x(4)
+        regroup_x(4, "gpsimd")
         project_v(3, 0)
         project_v(3, 1)
 
@@ -466,7 +475,7 @@ def tile_cross_module_pa_t_kernel(tc, x1, wq1, bq1, wv1, bv1, k2, out):
             gate_rows(s + 1, 0)
             gate_rows(s + 1, 1)
             if s + 3 < B:
-                regroup_x(s + 3)
+                regroup_x(s + 3, "gpsimd")
 
         last = B - 1
         quantise_gate(last - 2)
@@ -482,8 +491,7 @@ def tile_cross_module_pa_t_kernel(tc, x1, wq1, bq1, wv1, bv1, k2, out):
         regroup_gate(last - 1, "scalar", 0, 1)
         regroup_gate(last - 1, "scalar", 2, 3)
         gate_rows(last, 0)
-        for i in range(3):
-            keep_clock("q1")
+        keep_clock("q1", 3)
         transpose_gate(last, "gateT0", 0, 1)
         quantise_gate(last - 1)
         multiply(last - 1)

@@ -78,10 +78,15 @@ def tile_cross_module_pa_t_kernel(tc, x1, wq1, bq1, wv1, bv1, k2, out):
         nc.sync.dma_start(out=spread_rows[0:1, 2, 0:C2], in_=bv1.unsqueeze(0))
         load_x(1)
         load_x(2)
-        load_k2(2, 4)
         load_x(3)
-        load_k2(4, B)
-        for b in range(4, B):
+        load_k2(2, 4)
+        load_x(4)
+        load_x(5)
+        load_k2(4, 8)
+        load_x(6)
+        load_x(7)
+        load_k2(8, B)
+        for b in range(8, B):
             load_x(b)
 
         ident_f32 = const.tile([P, P], F32)
@@ -144,7 +149,7 @@ def tile_cross_module_pa_t_kernel(tc, x1, wq1, bq1, wv1, bv1, k2, out):
 
         x_buffers = [
             const.tile([P, N, PACK], BF16, align_bytes=64, name="x_buffer%d" % i)
-            for i in range(FIRST_BATCHES + 1)
+            for i in range(FIRST_BATCHES)
         ]
         x_codes, x_scales = {}, {}
         q, q_hi_biased, q_max, q_maxT, neg_q1 = {}, {}, {}, {}, {}
@@ -153,7 +158,7 @@ def tile_cross_module_pa_t_kernel(tc, x1, wq1, bq1, wv1, bv1, k2, out):
         product = {}
 
         def x_buffer(b):
-            return x_buffers[min(b, FIRST_BATCHES)]
+            return x_buffers[min(b, FIRST_BATCHES - 1)]
 
         def regroup_x(b, engine, part=WHOLE):
             xg = x_buffer(b)[:, part, :]

from contextlib import ExitStack

import concourse.mybir as mybir
from concourse.masks import make_identity

F32 = mybir.dt.float32
BF16 = mybir.dt.bfloat16
U32 = mybir.dt.uint32
U8 = mybir.dt.uint8
FP8X4 = mybir.dt.float8_e4m3fn_x4
ACT = mybir.ActivationFunctionType
ALU = mybir.AluOpType
AXIS = mybir.AxisListType

B = 16
C = 512
C2 = 256
N = 512
P = 128
PACK = 4
TILES = N // P
HALVES = C2 // P
WORDS = C // 2
WHOLE, LEFT, RIGHT = slice(0, N), slice(0, N // 2), slice(N // 2, N)
FIRST_BATCHES = 4
SPREAD = 3

FLOPS = 2 * B * (2 * C2 * C * N + C2 * N * N)


def tile_cross_module_pa_t_kernel(tc, x1, wq1, bq1, wv1, bv1, k2, out):
    nc = tc.nc
    with ExitStack() as stack:
        stack.enter_context(tc.manual_schedule())
        const = stack.enter_context(tc.tile_pool(name="const", bufs=1))
        xin = stack.enter_context(tc.tile_pool(name="xin", bufs=B))
        work = stack.enter_context(tc.tile_pool(name="work", bufs=2))

        warm = const.tile([P, 1], F32)
        nc.vector.memset(warm[:], 0.0)
        nc.scalar.activation(out=warm[:], in_=warm[:], func=ACT.Sigmoid)

        zeros = const.tile([P, N], BF16)
        nc.vector.memset(zeros[:].bitcast(U32), 0)
        bias_rows = const.tile([P, P], BF16)
        nc.vector.memset(bias_rows[:].bitcast(U32), 0)
        spread_rows = const.tile([P, SPREAD, N], BF16)
        nc.vector.memset(spread_rows[:].rearrange("p r n -> p (r n)").bitcast(U32), 0)
        w_rows = const.tile([P, 2 * HALVES, C], BF16)
        bv_all = const.tile([P, C2], BF16)
        k2_all = const.tile([P, B, N], BF16)
        x_raw = {}

        def load_x(b):
            xr = xin.tile([P, PACK, N], BF16)
            rows = x1[b].rearrange("(u p e) h w -> p u e (h w)", u=2, e=2)
            if b == 0:
                for part in (LEFT, RIGHT):
                    for u in range(2):
                        nc.sync.dma_start(
                            out=xr[:, 2 * u : 2 * u + 2, part], in_=rows[:, u, :, part]
                        )
            else:
                nc.sync.dma_start(out=xr[:].rearrange("p (u e) n -> p u e n", u=2), in_=rows)
            x_raw[b] = xr

        def load_k2(first, last):
            nc.sync.dma_start(
                out=k2_all[:, first:last, :].rearrange("p b n -> p (b n)"),
                in_=k2[first:last].rearrange("b n -> (b n)").partition_broadcast(P),
            )

        nc.sync.dma_start(out=w_rows[:, 0:HALVES, :], in_=wq1.rearrange("(g o) c -> o g c", o=P))
        load_x(0)
        nc.sync.dma_start(out=w_rows[:, HALVES:, :], in_=wv1.rearrange("(g o) c -> o g c", o=P))
        nc.sync.dma_start(out=bias_rows[0:HALVES, :], in_=bq1.rearrange("(g o) -> g o", o=P))
        nc.sync.dma_start(out=spread_rows[0:1, 0:2, :], in_=k2[0:2].unsqueeze(0))
        nc.sync.dma_start(out=spread_rows[0:1, 2, 0:C2], in_=bv1.unsqueeze(0))
        load_x(1)
        load_x(2)
        load_x(3)
        load_k2(2, 4)
        load_x(4)
        load_x(5)
        load_k2(4, 8)
        load_x(6)
        load_x(7)
        load_k2(8, B)
        for b in range(8, B):
            load_x(b)

        ident_f32 = const.tile([P, P], F32)
        make_identity(nc, ident_f32[:])
        ident_bf16 = const.tile([P, P], BF16)
        make_identity(nc, ident_bf16[:])


        ones = const.tile([P, P], BF16)
        nc.vector.memset(ones[:], 1.0)

        w_grouped = const.tile([P, 2 * C2 * PACK], BF16, align_bytes=64)
        w_codes = const.tile([P, 2 * C2], U32, align_bytes=64)
        w_scales = const.tile([P, 2 * C2], U8, align_bytes=64)
        bq_cols = const.tile([P, HALVES], F32)

        psum = stack.enter_context(tc.psum_pool(name="psum", bufs=1))

        def keep_clock(tag, count):
            for i in range(count):
                idle = psum.tile([P, N], F32, tag=tag)
                nc.tensor.matmul(
                    out=idle[:], lhsT=zeros[:, 0:P], rhs=zeros[:], start=True, stop=True
                )

        def transpose_weights(i):
            w_words = w_rows[:].rearrange("o g c -> o (g c)").bitcast(F32)
            grouped_words = w_grouped[:].bitcast(F32).rearrange("p (col u) -> p col u", u=2)
            wT = psum.tile([P, 2, C2], F32, tag="gateT%d" % i, name="wT%d" % i)
            for g in range(HALVES):
                for u in range(2):
                    first = (i * HALVES + g) * WORDS + u * P
                    nc.tensor.transpose(
                        wT[:, u, g * P : (g + 1) * P], w_words[:, first : first + P], ident_f32[:]
                    )
            nc.scalar.copy(
                out=grouped_words[:, i * C2 : (i + 1) * C2, :],
                in_=wT[:].rearrange("p u col -> p col u"),
            )

        def quantise_weights(i):
            cols = slice(i * C2, (i + 1) * C2)
            nc.vector.quantize_mx(
                out=w_codes[:, cols].bitcast(FP8X4),
                scales=w_scales[:, cols],
                in_=w_grouped[:, i * C2 * PACK : (i + 1) * C2 * PACK],
            )

        def transpose_bq():
            bqT = psum.tile([P, P], BF16, tag="out0")
            nc.tensor.transpose(bqT[:], bias_rows[:], ident_bf16[:])
            nc.scalar.copy(out=bq_cols[:], in_=bqT[:, 0:HALVES])

        def spread(row, width, tag, to):
            sp = psum.tile([P, width], BF16, tag=tag, name="spread%d" % row)
            nc.tensor.matmul(
                out=sp[:], lhsT=ones[:], rhs=spread_rows[:, row, 0:width], start=True, stop=True
            )
            nc.scalar.copy(out=to, in_=sp[:])

        x_buffers = [
            const.tile([P, N, PACK], BF16, align_bytes=64, name="x_buffer%d" % i)
            for i in range(FIRST_BATCHES)
        ]
        x_codes, x_scales = {}, {}
        q, q_hi_biased, q_max, q_maxT, neg_q1 = {}, {}, {}, {}, {}
        vT, v_grouped, v_codes, v_scales = {}, {}, {}, {}
        gate, gateT, gate_grouped, gate_codes, gate_scales = {}, {}, {}, {}, {}
        product = {}

        def x_buffer(b):
            return x_buffers[min(b, FIRST_BATCHES - 1)]

        def regroup_x(b, engine, part=WHOLE):
            xg = x_buffer(b)[:, part, :]
            xr = x_raw[b][:, :, part]
            if engine == "vector":
                nc.vector.tensor_copy(
                    out=xg.rearrange("p (c i) t -> p c t i", i=4),
                    in_=xr.rearrange("p t (c i) -> p c t i", i=4),
                )
            elif engine == "scalar":
                nc.scalar.copy(out=xg, in_=xr.rearrange("p t n -> p n t"))
            else:
                nc.gpsimd.tensor_scalar(
                    out=xg,
                    in0=xr.rearrange("p t n -> p n t"),
                    scalar1=1.0,
                    scalar2=0.0,
                    op0=ALU.mult,
                    op1=ALU.add,
                )

        def quantise_x(b, part=WHOLE):
            if b not in x_codes:
                xc = work.tile([P, N], U32, align_bytes=64)
                xs = work.tile([P, N], U8, align_bytes=64)
                x_codes[b], x_scales[b] = xc, xs
            nc.vector.quantize_mx(
                out=x_codes[b][:, part].bitcast(FP8X4),
                scales=x_scales[b][:, part],
                in_=x_buffer(b)[:, part, :].rearrange("p n t -> p (n t)"),
            )

        def project_v(b, h):
            acc = psum.tile([P, TILES, P], F32, tag="vT%d" % h, name="vT%d" % h)
            w_cols = slice(C2 + h * P, C2 + (h + 1) * P)
            for t in range(TILES):
                x_cols = slice(t * P, (t + 1) * P)
                nc.tensor.matmul_mx(
                    out=acc[:, t, :],
                    lhsT=x_codes[b][:, x_cols].bitcast(FP8X4),
                    lhsT_scale=x_scales[b][:, x_cols],
                    rhs=w_codes[:, w_cols].bitcast(FP8X4),
                    rhs_scale=w_scales[:, w_cols],
                    start=True,
                    stop=True,
                )
            vT[b, h] = acc

        def q_tag(part, g):
            return ("out%d" if part == RIGHT else "q%d") % g

        def project_q(b, g, part=WHOLE):
            acc = psum.tile([P, N], F32, tag=q_tag(part, g), name="q%d" % g)
            cols = slice(g * P, (g + 1) * P)
            nc.tensor.matmul_mx(
                out=acc[:, part],
                lhsT=w_codes[:, cols].bitcast(FP8X4),
                lhsT_scale=w_scales[:, cols],
                rhs=x_codes[b][:, part].bitcast(FP8X4),
                rhs_scale=x_scales[b][:, part],
                start=True,
                stop=True,
            )
            q[b, g, part.start] = acc

        def bias_q_hi(b, part=WHOLE):
            qb = work.tile([P, N], F32)
            nc.scalar.activation(
                out=qb[:, part],
                in_=q[b, 1, part.start][:, part],
                func=ACT.Identity,
                bias=bq_cols[:, 1:2],
                scale=1.0,
            )
            q_hi_biased[b, part.start] = qb

        def max_of_halves(b, part=WHOLE):
            qm = work.tile([P, N], F32)
            nc.vector.scalar_tensor_tensor(
                out=qm[:, part],
                in0=q[b, 0, part.start][:, part],
                scalar=bq_cols[:, 0:1],
                in1=q_hi_biased[b, part.start][:, part],
                op0=ALU.add,
                op1=ALU.max,
            )
            q_max[b, part.start] = qm

        def transpose_q(b, part=WHOLE):
            qT = psum.tile([P, TILES, P], F32, tag=q_tag(part, 0))
            for t in range(part.start // P, part.stop // P):
                nc.tensor.transpose(
                    qT[:, t, :], q_max[b, part.start][:, t * P : (t + 1) * P], ident_f32[:]
                )
            q_maxT[b, part.start] = qT

        def max_over_channels(b, part=WHOLE):
            if b not in neg_q1:
                nq = work.tile([P, TILES], F32, bufs=3)
                neg_q1[b] = nq
            tiles = slice(part.start // P, part.stop // P)
            nc.vector.tensor_reduce(
                out=neg_q1[b][:, tiles],
                in_=q_maxT[b, part.start][:, tiles, :],
                axis=AXIS.X,
                op=ALU.max,
                negate=True,
            )

        def bias_v(b, h):
            if h == 0:
                vg = work.tile([P, C2, PACK], BF16, align_bytes=64)
                v_grouped[b] = vg
            cols = slice(h * P, (h + 1) * P)
            nc.vector.tensor_tensor(
                out=v_grouped[b][:, cols, :],
                in0=vT[b, h][:].rearrange("p t c -> p c t"),
                in1=bv_all[:, cols].unsqueeze(2).to_broadcast([P, P, PACK]),
                op=ALU.add,
            )

        def quantise_v(b):
            vc = work.tile([P, C2], U32, align_bytes=64, bufs=3)
            vs = work.tile([P, C2], U8, align_bytes=64, bufs=3)
            nc.vector.quantize_mx(
                out=vc[:].bitcast(FP8X4),
                scales=vs[:],
                in_=v_grouped[b][:].rearrange("p c t -> p (c t)"),
            )
            v_codes[b], v_scales[b] = vc, vs

        def gate_rows(b, h):
            if h == 0:
                ga = work.tile([P, TILES, N], BF16)
                gate[b] = ga
            for t in (2 * h, 2 * h + 1):
                nc.scalar.activation(
                    out=gate[b][:, t, :].rearrange("p (u q e) -> p u q e", u=2, e=2),
                    in_=k2_all[:, b, :].rearrange("p (u e q) -> p u q e", u=2, e=2),
                    func=ACT.Sigmoid,
                    scale=neg_q1[b][:, t : t + 1],
                )

        def transpose_gate(b, tag, *tiles):
            words = gate[b][:].rearrange("p t k -> p (t k)").bitcast(F32)
            gT = psum.tile([P, 2, 2 * P], F32, tag=tag, name="gateT_" + tag)
            for j, t in enumerate(tiles):
                for u in range(2):
                    first = t * WORDS + u * P
                    nc.tensor.transpose(
                        gT[:, u, j * P : (j + 1) * P], words[:, first : first + P], ident_f32[:]
                    )
            gateT[b, tiles] = gT

        def copy_on(engine, **operands):
            if engine == "scalar":
                nc.scalar.copy(**operands)
            else:
                nc.vector.tensor_copy(**operands)

        def regroup_gate(b, engine, *tiles):
            if b not in gate_grouped:
                gg = work.tile([P, N * PACK], BF16, align_bytes=64)
                gate_grouped[b] = gg
            words = gate_grouped[b][:].bitcast(F32).rearrange("p (m u) -> p m u", u=2)
            copy_on(
                engine,
                out=words[:, tiles[0] * P : (tiles[-1] + 1) * P, :],
                in_=gateT[b, tiles][:, :, 0 : len(tiles) * P].rearrange("p u m -> p m u"),
            )

        def quantise_gate(b, first=0, last=N):
            if first == 0:
                gc = work.tile([P, N], U32, align_bytes=64)
                gs = work.tile([P, N], U8, align_bytes=64)
                gate_codes[b], gate_scales[b] = gc, gs
            nc.vector.quantize_mx(
                out=gate_codes[b][:, first:last].bitcast(FP8X4),
                scales=gate_scales[b][:, first:last],
                in_=gate_grouped[b][:, first * PACK : last * PACK],
            )

        def multiply(b, first=0, last=N):
            for g in range(HALVES):
                if first == 0:
                    tag = ("vT%d" if b == B - 1 else "out%d") % g
                    acc = psum.tile([P, N], F32, tag=tag, name="product%d" % g)
                    product[b, g] = acc
                cols = slice(g * P, (g + 1) * P)
                nc.tensor.matmul_mx(
                    out=product[b, g][:, first:last],
                    lhsT=v_codes[b][:, cols].bitcast(FP8X4),
                    lhsT_scale=v_scales[b][:, cols],
                    rhs=gate_codes[b][:, first:last].bitcast(FP8X4),
                    rhs_scale=gate_scales[b][:, first:last],
                    start=True,
                    stop=True,
                )

        def store(b, g, engine, first=0, last=N):
            res = work.tile([P, N], F32, bufs=8)
            copy_on(engine, out=res[:, first:last], in_=product[b, g][:, first:last])
            nc.sync.dma_start(
                out=out[b, g * P : (g + 1) * P].rearrange("c h w -> c (h w)")[:, first:last],
                in_=res[:, first:last],
            )

        def project(b):
            project_q(b, 1)
            project_v(b, 0)
            project_v(b, 1)
            project_q(b, 0)

        keep_clock("vT0", 3)
        regroup_x(0, "vector", LEFT)
        transpose_weights(0)
        keep_clock("vT0", 2)
        regroup_x(0, "vector", RIGHT)
        quantise_weights(0)
        transpose_bq()
        quantise_x(0, LEFT)
        quantise_x(0, RIGHT)
        transpose_weights(1)
        project_q(0, 1, LEFT)
        bias_q_hi(0, LEFT)
        project_q(0, 0, LEFT)
        project_q(0, 1, RIGHT)
        bias_q_hi(0, RIGHT)
        project_q(0, 0, RIGHT)
        regroup_x(1, "vector", LEFT)
        max_of_halves(0, LEFT)
        spread(0, N, "gateT0", k2_all[:, 0, :])
        transpose_q(0, LEFT)
        max_of_halves(0, RIGHT)
        transpose_q(0, RIGHT)
        max_over_channels(0, LEFT)
        gate_rows(0, 0)
        max_over_channels(0, RIGHT)
        quantise_weights(1)
        spread(2, C2, "out1", bv_all[:])
        gate_rows(0, 1)
        regroup_x(1, "vector", RIGHT)
        quantise_x(1)
        project_v(0, 0)
        project_v(0, 1)

        project_q(1, 1)
        project_q(1, 0)
        transpose_gate(0, "gateT0", 0, 1)
        bias_q_hi(1)
        regroup_gate(0, "scalar", 0, 1)
        spread(1, N, "out1", k2_all[:, 1, :])
        transpose_gate(0, "gateT1", 2, 3)
        bias_v(0, 0)
        regroup_x(2, "vector")
        max_of_halves(1)
        transpose_q(1)
        bias_v(0, 1)
        regroup_gate(0, "scalar", 2, 3)
        regroup_x(3, "scalar", RIGHT)
        project_v(1, 0)
        quantise_x(2)
        max_over_channels(1)
        project_q(2, 1)
        quantise_v(0)
        project_v(1, 1)
        project_q(2, 0)
        gate_rows(1, 0)
        bias_q_hi(2)
        gate_rows(1, 1)

        quantise_gate(0)
        multiply(0)
        regroup_x(3, "vector", LEFT)
        bias_v(1, 0)
        bias_v(1, 1)
        quantise_x(3)
        quantise_v(1)
        transpose_gate(1, "gateT0", 0, 1)
        max_of_halves(2)
        transpose_gate(1, "gateT1", 2, 3)
        project_q(3, 1)
        transpose_q(2)
        store(0, 1, "vector")
        max_over_channels(2)
        project_v(2, 0)
        project_v(2, 1)
        regroup_gate(1, "scalar", 0, 1)
        store(0, 0, "scalar")
        regroup_gate(1, "scalar", 2, 3)
        bias_q_hi(3)
        bias_v(2, 0)
        bias_v(2, 1)
        project_q(3, 0)
        gate_rows(2, 0)
        gate_rows(2, 1)
        regroup_x(4, "gpsimd")
        project_v(3, 0)
        project_v(3, 1)

        for s in range(2, B - 2):
            quantise_gate(s - 1)
            multiply(s - 1)
            quantise_x(s + 2)
            quantise_v(s)
            max_of_halves(s + 1)
            transpose_gate(s, "gateT0", 0, 1)
            transpose_q(s + 1)
            transpose_gate(s, "gateT1", 2, 3)
            bias_v(s + 1, 0)
            bias_v(s + 1, 1)
            max_over_channels(s + 1)
            regroup_gate(s, "scalar", 0, 1)
            store(s - 1, 0, "scalar")
            regroup_gate(s, "scalar", 2, 3)
            store(s - 1, 1, "vector")
            project(s + 2)
            bias_q_hi(s + 2)
            gate_rows(s + 1, 0)
            gate_rows(s + 1, 1)
            if s + 3 < B:
                regroup_x(s + 3, "gpsimd")

        last = B - 1
        quantise_gate(last - 2)
        multiply(last - 2)
        quantise_v(last - 1)
        max_of_halves(last)
        transpose_gate(last - 1, "gateT0", 0, 1)
        transpose_q(last)
        transpose_gate(last - 1, "gateT1", 2, 3)
        store(last - 2, 0, "vector")
        max_over_channels(last)
        store(last - 2, 1, "vector")
        regroup_gate(last - 1, "scalar", 0, 1)
        regroup_gate(last - 1, "scalar", 2, 3)
        gate_rows(last, 0)
        keep_clock("q1", 3)
        transpose_gate(last, "gateT0", 0, 1)
        quantise_gate(last - 1)
        multiply(last - 1)
        bias_v(last, 0)
        bias_v(last, 1)
        quantise_v(last)
        gate_rows(last, 1)
        transpose_gate(last, "gateT1", 2)
        transpose_gate(last, "q0", 3)
        regroup_gate(last, "scalar", 0, 1)
        store(last - 1, 0, "scalar")
        regroup_gate(last, "vector", 2)
        regroup_gate(last, "scalar", 3)
        quantise_gate(last, 0, N // 2)
        multiply(last, 0, N // 2)
        quantise_gate(last, N // 2, N)
        store(last - 1, 1, "scalar")
        store(last, 1, "vector", 0, N // 2)
        store(last, 0, "scalar", 0, N // 2)
        multiply(last, N // 2, N)
        store(last, 1, "vector", N // 2, N)
        store(last, 0, "scalar", N // 2, N)
